import numpy as np
import ml_dtypes


def mxq(x, axis, fmt="e4m3"):
    dtype, down = {"e4m3": (ml_dtypes.float8_e4m3fn, 7), "e5m2": (ml_dtypes.float8_e5m2, 14)}[fmt]
    v = np.moveaxis(np.asarray(x, np.float32).astype(ml_dtypes.bfloat16).astype(np.float64), axis, -1)
    blocks = v.reshape(v.shape[:-1] + (-1, 32))
    amax = np.abs(blocks).max(-1, keepdims=True)
    byte = np.maximum(np.where(amax > 0, np.frexp(amax)[1] - 1 + 127, 0) - down, 1)
    scale = np.exp2(byte - 127.0)
    codes = (blocks / scale).astype(np.float32).astype(dtype).astype(np.float64)
    return np.moveaxis((codes * scale).reshape(v.shape), -1, axis)


WIDE = False


def mx_kscale(k):
    if not WIDE:
        return np.ones(k)
    levels = np.array([10, -10, 5, -5, 0])
    a = np.random.permutation(np.resize(levels, k // 512 * 4)).reshape(k // 512, 4)
    idx = np.arange(k)
    return np.exp2(a[idx // 512, idx % 128 // 32])


BF16 = ml_dtypes.bfloat16


def bf(x):
    return np.asarray(x, np.float32).astype(BF16)


def f64(x):
    return np.asarray(x).astype(np.float64)


N, CI, CO, H, W, KH, KW = 4, 128, 256, 66, 66, 3, 3
HO, WO = H - KH + 1, W - KW + 1
L = N * HO * WO


def setup_inputs():
    u = np.unique(mx_kscale(L))
    sn = u[(np.arange(N) * (len(u) - 1)) % len(u)][:, None, None, None]
    return {"input": bf(np.random.standard_normal((N, CI, H, W)) / sn),
            "grad_output": bf(np.random.standard_normal((N, CO, HO, WO)) / np.sqrt(L) * sn)}


def reference(input, grad_output):
    x = f64(input)
    gq = mxq(f64(grad_output).transpose(1, 0, 2, 3).reshape(CO, L), 1, "e4m3")
    taps = []
    for i in range(KH):
        for j in range(KW):
            patch = x[:, :, i:i + HO, j:j + WO].transpose(1, 0, 2, 3).reshape(CI, L)
            taps.append(gq @ mxq(patch, 1, "e4m3").T)
    return np.stack(taps, axis=-1).reshape(CO, CI, KH, KW)

@@ -1,0 +1,236 @@
+from contextlib import ExitStack
+
+import concourse.mybir as mybir
+from concourse.masks import make_identity
+
+F32 = mybir.dt.float32
+BF16 = mybir.dt.bfloat16
+U32 = mybir.dt.uint32
+U8 = mybir.dt.uint8
+FP8X4 = mybir.dt.float8_e4m3fn_x4
+
+P = 128
+N_IMG = 4
+CI = 128
+CO = 256
+W_IN = 66
+W_OUT = 64
+HALF = 32
+PASSES = 32
+UNITS = 34
+XW = W_IN // 2
+GW = W_OUT // 2
+G_CUTS = [0, 2, 4, 8, 12, 16, 20, 24, 28, 32]
+N_CHUNKS = 9
+X_CUTS = [0, 4, 6, 10, 14, 18, 22, 26, 30, 34]
+AHEAD = 4
+ROUNDS = PASSES // 2
+TAPW = 3 * CI
+
+FLOPS = 2 * CO * CI * 9 * N_IMG * W_OUT * W_OUT
+
+
+def tile_model_pa_kernel(tc, x, g, out):
+    nc = tc.nc
+    with ExitStack() as ctx:
+        keep = ctx.enter_context(tc.tile_pool(name="keep", bufs=1))
+        gn_pool = ctx.enter_context(tc.tile_pool(name="gn", bufs=AHEAD))
+        rl_pool = ctx.enter_context(tc.tile_pool(name="rl", bufs=2))
+        gr_pool = ctx.enter_context(tc.tile_pool(name="grp", bufs=3))
+        acc_pool = ctx.enter_context(tc.psum_pool(name="acc", bufs=1))
+        tp_pool = ctx.enter_context(tc.psum_pool(name="tp", bufs=1))
+        ctx.enter_context(tc.manual_schedule())
+
+        ident = keep.tile([P, P], F32, name="ident")
+        make_identity(nc, ident[:])
+
+        g_codes = keep.tile([P, PASSES * CO], U32, name="g_codes", align_bytes=64)
+        g_scales = keep.tile([P, PASSES * CO], U8, name="g_scales", align_bytes=64)
+        x_codes = keep.tile([P, UNITS * TAPW], U32, name="x_codes", align_bytes=64)
+        x_scales = keep.tile([P, UNITS * TAPW], U8, name="x_scales", align_bytes=64)
+        acc = [[acc_pool.tile([P, 512], F32, name="acc%d%d" % (h, s)) for s in range(2)] for h in range(2)]
+
+        gn_tiles = {}
+        xn_tiles = {}
+        stage = {}
+
+        def load_chunk(c):
+            u0, u1 = X_CUTS[c], X_CUTS[c + 1]
+            run = (u1 - u0) * W_IN
+            xn = gn_pool.tile([P, N_IMG, 2, (run + 15) // 16 * 16], BF16, name="xn")
+            xn_tiles[c] = xn
+            for a in range(2):
+                nc.sync.dma_start(
+                    out=xn[:, :, a, 0:run],
+                    in_=x[:, :, HALF * a + u0 : HALF * a + u1, :].rearrange("n c h w -> c n (h w)"),
+                )
+            r0, r1 = G_CUTS[c], G_CUTS[c + 1]
+            gn = gn_pool.tile([P, 2, N_IMG, 2, (r1 - r0) * W_OUT], BF16, name="gn")
+            gn_tiles[c] = gn
+            for h in range(2):
+                for a in range(2):
+                    nc.sync.dma_start(
+                        out=gn[:, h, :, a, :],
+                        in_=g[:, P * h : P * (h + 1), HALF * a + r0 : HALF * a + r1, :].rearrange(
+                            "n c h w -> c n (h w)"
+                        ),
+                    )
+
+        def chunk_of(cuts, first):
+            return max(c for c in range(N_CHUNKS) if cuts[c] <= first)
+
+        def has_g(it):
+            return 0 <= it < ROUNDS
+
+        def exists(it):
+            return -1 <= it < ROUNDS
+
+        def relayout(it):
+            st = {}
+            stage[it] = st
+            if has_g(it):
+                c = chunk_of(G_CUTS, 2 * it)
+                l0 = 2 * it - G_CUTS[c]
+                gn_w = gn_tiles[c][:].bitcast(F32)
+                gr = rl_pool.tile([P, 2, 2, 2, P], F32, name="gr")
+                st["gr"] = gr
+                for h in range(2):
+                    nc.vector.tensor_copy(
+                        out=gr[:, :, h, :, :].rearrange("p i w (x b) -> p i w x b", b=16),
+                        in_=gn_w[:, h, :, :, l0 * GW : (l0 + 2) * GW].rearrange(
+                            "p n a (i b w) -> p i w (n a) b", i=2, b=16, w=2
+                        ),
+                    )
+            c = chunk_of(X_CUTS, 2 * (it + 1))
+            u0 = 2 * (it + 1) - X_CUTS[c]
+            xr = rl_pool.tile([P, 2, 3, P], F32, name="xr")
+            st["xr"] = xr
+            rows = xn_tiles[c][:].bitcast(F32)[:, :, :, u0 * XW : (u0 + 2) * XW].rearrange("p n a (u k) -> p u (n a) k", u=2, k=XW)
+            nc.vector.tensor_copy(
+                out=xr[:, :, 0:2, :].rearrange("p u w (x b) -> p u w x b", b=16),
+                in_=rows[:, :, :, 0:32].rearrange("p u x (b w) -> p u w x b", w=2),
+            )
+            nc.vector.tensor_copy(
+                out=xr[:, :, 2, :].rearrange("p u (x b) -> p u x b", b=16),
+                in_=rows[:, :, :, 2:33:2],
+            )
+
+        def transposes(it):
+            st = stage[it]
+            if has_g(it):
+                st["gb"] = []
+                for li in range(2):
+                    gb = tp_pool.tile([P, 512], F32, name="gb%d" % li)
+                    st["gb"].append(gb)
+                    for w in range(2):
+                        for h in range(2):
+                            k = 2 * w + h
+                            nc.tensor.transpose(gb[:, k * P : (k + 1) * P], st["gr"][:, li, h, w, :], ident[:])
+            st["xb"] = []
+            for lu in range(2):
+                xb = tp_pool.tile([P, 512], F32, name="xb%d" % lu)
+                st["xb"].append(xb)
+                for w in range(3):
+                    nc.tensor.transpose(xb[:, w * P : (w + 1) * P], st["xr"][:, lu, w, :], ident[:])
+
+        def copies(it):
+            st = stage[it]
+            if has_g(it):
+                gg = gr_pool.tile([P, 2, CO, 4], BF16, name="gg", align_bytes=64)
+                st["gg"] = gg
+                gg_w = gg[:].bitcast(F32)
+                for li in range(2):
+                    nc.scalar.copy(out=gg_w[:, li], in_=st["gb"][li][:].rearrange("p (w c) -> p c w", w=2))
+            xg = gr_pool.tile([P, 2, 3, CI, 4], BF16, name="xg", align_bytes=64)
+            st["xg"] = xg
+            xg_w = xg[:].bitcast(F32)
+            for lu in range(2):
+                for k in range(2):
+                    nc.scalar.copy(
+                        out=xg_w[:, lu, 2 * k],
+                        in_=st["xb"][lu][:, k * P : (k + 2) * P].rearrange("p (w c) -> p c w", w=2),
+                    )
+
+        def quantise(it):
+            st = stage[it]
+            xg = st["xg"]
+            nc.vector.tensor_copy(
+                out=xg[:, :, 1, :, :].rearrange("p u c (k e) -> p u c k e", k=2),
+                in_=xg[:, :, 0:3:2, :, 1:3].rearrange("p u k c e -> p u c k e"),
+            )
+            if has_g(it):
+                c0 = 2 * it * CO
+                nc.vector.quantize_mx(
+                    out=g_codes[:, c0 : c0 + 2 * CO].bitcast(FP8X4),
+                    scales=g_scales[:, c0 : c0 + 2 * CO],
+                    in_=st["gg"][:].rearrange("p i c t -> p (i c t)"),
+                )
+            flat = xg[:].rearrange("p u k c t -> p (u k c t)")
+            c0 = 2 * (it + 1) * TAPW
+            nc.vector.quantize_mx(
+                out=x_codes[:, c0 : c0 + 512].bitcast(FP8X4),
+                scales=x_scales[:, c0 : c0 + 512],
+                in_=flat[:, 0:2048],
+            )
+            nc.vector.quantize_mx(
+                out=x_codes[:, c0 + 512 : c0 + 768].bitcast(FP8X4),
+                scales=x_scales[:, c0 + 512 : c0 + 768],
+                in_=flat[:, 2048:3072],
+            )
+
+        def mx_pass(dst, r, h, col, width):
+            gc = r * CO + h * P
+            xc = r * TAPW + col
+            nc.tensor.matmul_mx(
+                out=dst,
+                lhsT=g_codes[:, gc : gc + P].bitcast(FP8X4),
+                lhsT_scale=g_scales[:, gc : gc + P],
+                rhs=x_codes[:, xc : xc + width].bitcast(FP8X4),
+                rhs_scale=x_scales[:, xc : xc + width],
+                start=(r == 0),
+                stop=(r == PASSES - 1),
+            )
+
+        def multiply(rd):
+            for r in (2 * rd, 2 * rd + 1):
+                for h in range(2):
+                    for s in range(2):
+                        mx_pass(acc[h][s][:], r, h, 512 * s, 512)
+
+        for c in range(AHEAD):
+            load_chunk(c)
+        for it in range(-2, ROUNDS + 2):
+            if exists(it + 1):
+                relayout(it + 1)
+                done = 2 * (it + 1) + 2
+                if done in G_CUTS[1:] and G_CUTS.index(done) - 1 + AHEAD < N_CHUNKS:
+                    load_chunk(G_CUTS.index(done) - 1 + AHEAD)
+            if exists(it):
+                transposes(it)
+            if has_g(it - 2):
+                multiply(it - 2)
+            if exists(it):
+                copies(it)
+            if exists(it - 1):
+                quantise(it - 1)
+
+        res = [keep.tile([P, CI, 9], F32, name="res%d" % h) for h in range(2)]
+        last = tp_pool.tile([P, 512], F32, name="gb0")
+
+        def leave(h, dst, src):
+            if h == 0:
+                nc.vector.tensor_copy(out=dst, in_=src)
+            else:
+                nc.scalar.copy(out=dst, in_=src)
+
+        for h in range(2):
+            for s in range(2):
+                leave(h, res[h][:, :, 4 * s : 4 * s + 4], acc[h][s][:].rearrange("p (t c) -> p c t", t=4))
+        for h in range(2):
+            for r in range(PASSES):
+                mx_pass(last[:, h * P : (h + 1) * P], r, h, 1024, P)
+            leave(h, res[h][:, :, 8:9], last[:, h * P : (h + 1) * P].rearrange("p (c o) -> p c o", o=1))
+            nc.sync.dma_start(
+                out=out[h * P : (h + 1) * P].rearrange("o c kh kw -> o (c kh kw)"),
+                in_=res[h][:].rearrange("p c t -> p (c t)"),
+            )

@@ -106,14 +106,11 @@ def tile_model_pa_kernel(tc, x, g, out):
             xr = rl_pool.tile([P, 2, 3, P], F32, name="xr")
             st["xr"] = xr
             rows = xn_tiles[c][:].bitcast(F32)[:, :, :, u0 * XW : (u0 + 2) * XW].rearrange("p n a (u k) -> p u (n a) k", u=2, k=XW)
-            nc.vector.tensor_copy(
-                out=xr[:, :, 0:2, :].rearrange("p u w (x b) -> p u w x b", b=16),
-                in_=rows[:, :, :, 0:32].rearrange("p u x (b w) -> p u w x b", w=2),
-            )
-            nc.vector.tensor_copy(
-                out=xr[:, :, 2, :].rearrange("p u (x b) -> p u x b", b=16),
-                in_=rows[:, :, :, 2:33:2],
-            )
+            for w in range(3):
+                nc.scalar.copy(
+                    out=xr[:, :, w, :].rearrange("p u (x b) -> p u x b", b=16),
+                    in_=rows[:, :, :, w : w + 31 : 2],
+                )
 
         def transposes(it):
             st = stage[it]

@@ -20,9 +20,9 @@ PASSES = 32
 UNITS = 34
 XW = W_IN // 2
 GW = W_OUT // 2
-G_CUTS = [0, 2, 4, 8, 12, 16, 20, 24, 28, 32]
-N_CHUNKS = 9
-X_CUTS = [0, 4, 6, 10, 14, 18, 22, 26, 30, 34]
+G_CUTS = [0, 2, 4, 6, 8, 10, 12, 16, 20, 24, 28, 32]
+N_CHUNKS = 11
+X_CUTS = [0, 4, 6, 8, 10, 12, 14, 18, 22, 26, 30, 34]
 AHEAD = 4
 ROUNDS = PASSES // 2
 TAPW = 3 * CI
@@ -106,11 +106,14 @@ def tile_model_pa_kernel(tc, x, g, out):
             xr = rl_pool.tile([P, 2, 3, P], F32, name="xr")
             st["xr"] = xr
             rows = xn_tiles[c][:].bitcast(F32)[:, :, :, u0 * XW : (u0 + 2) * XW].rearrange("p n a (u k) -> p u (n a) k", u=2, k=XW)
-            for w in range(3):
-                nc.scalar.copy(
-                    out=xr[:, :, w, :].rearrange("p u (x b) -> p u x b", b=16),
-                    in_=rows[:, :, :, w : w + 31 : 2],
-                )
+            nc.vector.tensor_copy(
+                out=xr[:, :, 0:2, :].rearrange("p u w (x b) -> p u w x b", b=16),
+                in_=rows[:, :, :, 0:32].rearrange("p u x (b w) -> p u w x b", w=2),
+            )
+            nc.vector.tensor_copy(
+                out=xr[:, :, 2, :].rearrange("p u (x b) -> p u x b", b=16),
+                in_=rows[:, :, :, 2:33:2],
+            )
 
         def transposes(it):
             st = stage[it]
@@ -197,6 +200,8 @@ def tile_model_pa_kernel(tc, x, g, out):
         for c in range(AHEAD):
             load_chunk(c)
         for it in range(-2, ROUNDS + 2):
+            if exists(it - 1):
+                quantise(it - 1)
             if exists(it + 1):
                 relayout(it + 1)
                 done = 2 * (it + 1) + 2
@@ -208,8 +213,6 @@ def tile_model_pa_kernel(tc, x, g, out):
                 multiply(it - 2)
             if exists(it):
                 copies(it)
-            if exists(it - 1):
-                quantise(it - 1)
 
         res = [keep.tile([P, CI, 9], F32, name="res%d" % h) for h in range(2)]
         last = tp_pool.tile([P, 512], F32, name="gb0")

@@ -154,10 +154,6 @@ def tile_model_pa_kernel(tc, x, g, out):
         def quantise(it):
             st = stage[it]
             xg = st["xg"]
-            nc.vector.tensor_copy(
-                out=xg[:, :, 1, :, :].rearrange("p u c (k e) -> p u c k e", k=2),
-                in_=xg[:, :, 0:3:2, :, 1:3].rearrange("p u k c e -> p u c k e"),
-            )
             if has_g(it):
                 c0 = 2 * it * CO
                 nc.vector.quantize_mx(
@@ -165,6 +161,10 @@ def tile_model_pa_kernel(tc, x, g, out):
                     scales=g_scales[:, c0 : c0 + 2 * CO],
                     in_=st["gg"][:].rearrange("p i c t -> p (i c t)"),
                 )
+            nc.vector.tensor_copy(
+                out=xg[:, :, 1, :, :].rearrange("p u c (k e) -> p u c k e", k=2),
+                in_=xg[:, :, 0:3:2, :, 1:3].rearrange("p u k c e -> p u c k e"),
+            )
             flat = xg[:].rearrange("p u k c t -> p (u k c t)")
             c0 = 2 * (it + 1) * TAPW
             nc.vector.quantize_mx(
@@ -199,7 +199,7 @@ def tile_model_pa_kernel(tc, x, g, out):
 
         for c in range(AHEAD):
             load_chunk(c)
-        for it in range(-2, ROUNDS + 2):
+        for it in range(-2, ROUNDS + 1):
             if exists(it - 1):
                 quantise(it - 1)
             if exists(it + 1):
@@ -209,8 +209,8 @@ def tile_model_pa_kernel(tc, x, g, out):
                     load_chunk(G_CUTS.index(done) - 1 + AHEAD)
             if exists(it):
                 transposes(it)
-            if has_g(it - 2):
-                multiply(it - 2)
+            if has_g(it - 1):
+                multiply(it - 1)
             if exists(it):
                 copies(it)
 

@@ -20,9 +20,9 @@ PASSES = 32
 UNITS = 34
 XW = W_IN // 2
 GW = W_OUT // 2
-G_CUTS = [0, 2, 4, 6, 8, 10, 12, 16, 20, 24, 28, 32]
-N_CHUNKS = 11
-X_CUTS = [0, 4, 6, 8, 10, 12, 14, 18, 22, 26, 30, 34]
+G_CUTS = [0, 2, 4, 8, 12, 16, 20, 24, 28, 32]
+N_CHUNKS = 9
+X_CUTS = [0, 4, 6, 10, 14, 18, 22, 26, 30, 34]
 AHEAD = 4
 ROUNDS = PASSES // 2
 TAPW = 3 * CI

@@ -22,7 +22,7 @@ XW = W_IN // 2
 GW = W_OUT // 2
 G_CUTS = [0, 2, 4, 8, 12, 16, 20, 24, 28, 32]
 N_CHUNKS = 9
-X_CUTS = [0, 4, 6, 10, 14, 18, 22, 26, 30, 34]
+X_CUTS = [0, 4, 8, 12, 16, 20, 24, 28, 32, 34]
 AHEAD = 4
 ROUNDS = PASSES // 2
 TAPW = 3 * CI
@@ -82,29 +82,30 @@ def tile_model_pa_kernel(tc, x, g, out):
         def has_g(it):
             return 0 <= it < ROUNDS
 
-        def exists(it):
-            return -1 <= it < ROUNDS
+        def has_x(it):
+            return -2 <= it < ROUNDS - 1
 
-        def relayout(it):
-            st = {}
-            stage[it] = st
-            if has_g(it):
-                c = chunk_of(G_CUTS, 2 * it)
-                l0 = 2 * it - G_CUTS[c]
-                gn_w = gn_tiles[c][:].bitcast(F32)
-                gr = rl_pool.tile([P, 2, 2, 2, P], F32, name="gr")
-                st["gr"] = gr
-                for h in range(2):
-                    nc.vector.tensor_copy(
-                        out=gr[:, :, h, :, :].rearrange("p i w (x b) -> p i w x b", b=16),
-                        in_=gn_w[:, h, :, :, l0 * GW : (l0 + 2) * GW].rearrange(
-                            "p n a (i b w) -> p i w (n a) b", i=2, b=16, w=2
-                        ),
-                    )
-            c = chunk_of(X_CUTS, 2 * (it + 1))
-            u0 = 2 * (it + 1) - X_CUTS[c]
+        def stage_of(it):
+            return stage.setdefault(it, {})
+
+        def sort_g(it):
+            c = chunk_of(G_CUTS, 2 * it)
+            l0 = 2 * it - G_CUTS[c]
+            gn_w = gn_tiles[c][:].bitcast(F32)
+            gr = rl_pool.tile([P, 2, 2, 2, P], F32, name="gr")
+            stage_of(it)["gr"] = gr
+            nc.vector.tensor_copy(
+                out=gr[:].rearrange("p i w h (x b) -> p i w (h x) b", b=16),
+                in_=gn_w[:, :, :, :, l0 * GW : (l0 + 2) * GW].rearrange(
+                    "p h n a (i b w) -> p i w (h n a) b", i=2, b=16, w=2
+                ),
+            )
+
+        def sort_x(it):
+            c = chunk_of(X_CUTS, 2 * it + 4)
+            u0 = 2 * it + 4 - X_CUTS[c]
             xr = rl_pool.tile([P, 2, 3, P], F32, name="xr")
-            st["xr"] = xr
+            stage_of(it)["xr"] = xr
             rows = xn_tiles[c][:].bitcast(F32)[:, :, :, u0 * XW : (u0 + 2) * XW].rearrange("p n a (u k) -> p u (n a) k", u=2, k=XW)
             nc.vector.tensor_copy(
                 out=xr[:, :, 0:2, :].rearrange("p u w (x b) -> p u w x b", b=16),
@@ -115,17 +116,19 @@ def tile_model_pa_kernel(tc, x, g, out):
                 in_=rows[:, :, :, 2:33:2],
             )
 
-        def transposes(it):
-            st = stage[it]
-            if has_g(it):
-                st["gb"] = []
-                for li in range(2):
-                    gb = tp_pool.tile([P, 512], F32, name="gb%d" % li)
-                    st["gb"].append(gb)
-                    for w in range(2):
-                        for h in range(2):
-                            k = 2 * w + h
-                            nc.tensor.transpose(gb[:, k * P : (k + 1) * P], st["gr"][:, li, h, w, :], ident[:])
+        def transpose_g(it):
+            st = stage_of(it)
+            st["gb"] = []
+            for li in range(2):
+                gb = tp_pool.tile([P, 512], F32, name="gb%d" % li)
+                st["gb"].append(gb)
+                for w in range(2):
+                    for h in range(2):
+                        k = 2 * w + h
+                        nc.tensor.transpose(gb[:, k * P : (k + 1) * P], st["gr"][:, li, w, h, :], ident[:])
+
+        def transpose_x(it):
+            st = stage_of(it)
             st["xb"] = []
             for lu in range(2):
                 xb = tp_pool.tile([P, 512], F32, name="xb%d" % lu)
@@ -133,14 +136,16 @@ def tile_model_pa_kernel(tc, x, g, out):
                 for w in range(3):
                     nc.tensor.transpose(xb[:, w * P : (w + 1) * P], st["xr"][:, lu, w, :], ident[:])
 
-        def copies(it):
-            st = stage[it]
-            if has_g(it):
-                gg = gr_pool.tile([P, 2, CO, 4], BF16, name="gg", align_bytes=64)
-                st["gg"] = gg
-                gg_w = gg[:].bitcast(F32)
-                for li in range(2):
-                    nc.scalar.copy(out=gg_w[:, li], in_=st["gb"][li][:].rearrange("p (w c) -> p c w", w=2))
+        def copy_g(it):
+            st = stage_of(it)
+            gg = gr_pool.tile([P, 2, CO, 4], BF16, name="gg", align_bytes=64)
+            st["gg"] = gg
+            gg_w = gg[:].bitcast(F32)
+            for li in range(2):
+                nc.scalar.copy(out=gg_w[:, li], in_=st["gb"][li][:].rearrange("p (w c) -> p c w", w=2))
+
+        def copy_x(it):
+            st = stage_of(it)
             xg = gr_pool.tile([P, 2, 3, CI, 4], BF16, name="xg", align_bytes=64)
             st["xg"] = xg
             xg_w = xg[:].bitcast(F32)
@@ -151,22 +156,24 @@ def tile_model_pa_kernel(tc, x, g, out):
                         in_=st["xb"][lu][:, k * P : (k + 2) * P].rearrange("p (w c) -> p c w", w=2),
                     )
 
-        def quantise(it):
-            st = stage[it]
-            xg = st["xg"]
-            if has_g(it):
-                c0 = 2 * it * CO
-                nc.vector.quantize_mx(
-                    out=g_codes[:, c0 : c0 + 2 * CO].bitcast(FP8X4),
-                    scales=g_scales[:, c0 : c0 + 2 * CO],
-                    in_=st["gg"][:].rearrange("p i c t -> p (i c t)"),
-                )
+        def middle_tap(it):
+            xg = stage_of(it)["xg"]
             nc.vector.tensor_copy(
                 out=xg[:, :, 1, :, :].rearrange("p u c (k e) -> p u c k e", k=2),
                 in_=xg[:, :, 0:3:2, :, 1:3].rearrange("p u k c e -> p u c k e"),
             )
-            flat = xg[:].rearrange("p u k c t -> p (u k c t)")
-            c0 = 2 * (it + 1) * TAPW
+
+        def quantise_g(it):
+            c0 = 2 * it * CO
+            nc.vector.quantize_mx(
+                out=g_codes[:, c0 : c0 + 2 * CO].bitcast(FP8X4),
+                scales=g_scales[:, c0 : c0 + 2 * CO],
+                in_=stage_of(it)["gg"][:].rearrange("p i c t -> p (i c t)"),
+            )
+
+        def quantise_x(it):
+            flat = stage_of(it)["xg"][:].rearrange("p u k c t -> p (u k c t)")
+            c0 = (2 * it + 4) * TAPW
             nc.vector.quantize_mx(
                 out=x_codes[:, c0 : c0 + 512].bitcast(FP8X4),
                 scales=x_scales[:, c0 : c0 + 512],
@@ -193,29 +200,47 @@ def tile_model_pa_kernel(tc, x, g, out):
 
         def multiply(rd):
             for r in (2 * rd, 2 * rd + 1):
-                for h in range(2):
-                    for s in range(2):
+                for s in range(2):
+                    for h in range(2):
                         mx_pass(acc[h][s][:], r, h, 512 * s, 512)
+
+        def last_tap(h, r0, r1):
+            for r in range(r0, r1):
+                mx_pass(last[h][:, 0:P], r, h, 1024, P)
 
         for c in range(AHEAD):
             load_chunk(c)
-        for it in range(-2, ROUNDS + 1):
-            if exists(it - 1):
-                quantise(it - 1)
-            if exists(it + 1):
-                relayout(it + 1)
-                done = 2 * (it + 1) + 2
-                if done in G_CUTS[1:] and G_CUTS.index(done) - 1 + AHEAD < N_CHUNKS:
-                    load_chunk(G_CUTS.index(done) - 1 + AHEAD)
-            if exists(it):
-                transposes(it)
+        for it in range(-3, ROUNDS + 1):
+            if has_g(it - 1):
+                quantise_g(it - 1)
+            if has_x(it - 1):
+                middle_tap(it - 1)
+            if has_x(it - 1) and it <= 0:
+                quantise_x(it - 1)
+            if has_g(it + 1):
+                sort_g(it + 1)
+            if has_x(it - 1) and it > 0:
+                quantise_x(it - 1)
+            if has_x(it + 1):
+                sort_x(it + 1)
+            done = 2 * (it + 1) + 2
+            if done in G_CUTS[1:] and G_CUTS.index(done) - 1 + AHEAD < N_CHUNKS:
+                load_chunk(G_CUTS.index(done) - 1 + AHEAD)
+            if has_g(it):
+                transpose_g(it)
+            if has_x(it):
+                transpose_x(it)
+            if it == ROUNDS:
+                last = [tp_pool.tile([P, 512], F32, name="xb%d" % h) for h in range(2)]
+                last_tap(0, 0, 8)
             if has_g(it - 1):
                 multiply(it - 1)
-            if exists(it):
-                copies(it)
+            if has_g(it):
+                copy_g(it)
+            if has_x(it):
+                copy_x(it)
 
         res = [keep.tile([P, CI, 9], F32, name="res%d" % h) for h in range(2)]
-        last = tp_pool.tile([P, 512], F32, name="gb0")
 
         def leave(h, dst, src):
             if h == 0:
@@ -223,14 +248,16 @@ def tile_model_pa_kernel(tc, x, g, out):
             else:
                 nc.scalar.copy(out=dst, in_=src)
 
-        for h in range(2):
-            for s in range(2):
+        for s in range(2):
+            for h in range(2):
                 leave(h, res[h][:, :, 4 * s : 4 * s + 4], acc[h][s][:].rearrange("p (t c) -> p c t", t=4))
+        last_tap(0, 8, PASSES)
+        last_tap(1, 0, PASSES)
         for h in range(2):
-            for r in range(PASSES):
-                mx_pass(last[:, h * P : (h + 1) * P], r, h, 1024, P)
-            leave(h, res[h][:, :, 8:9], last[:, h * P : (h + 1) * P].rearrange("p (c o) -> p c o", o=1))
-            nc.sync.dma_start(
-                out=out[h * P : (h + 1) * P].rearrange("o c kh kw -> o (c kh kw)"),
-                in_=res[h][:].rearrange("p c t -> p (c t)"),
-            )
+            for c0 in range(0, CI, CI // 2):
+                cs = slice(c0, c0 + CI // 2)
+                leave(h, res[h][:, cs, 8:9], last[h][:, cs].rearrange("p (c o) -> p c o", o=1))
+                nc.sync.dma_start(
+                    out=out[h * P : (h + 1) * P, cs].rearrange("o c kh kw -> o (c kh kw)"),
+                    in_=res[h][:, cs].rearrange("p c t -> p (c t)"),
+                )

@@ -158,10 +158,11 @@ def tile_model_pa_kernel(tc, x, g, out):
 
         def middle_tap(it):
             xg = stage_of(it)["xg"]
-            nc.vector.tensor_copy(
-                out=xg[:, :, 1, :, :].rearrange("p u c (k e) -> p u c k e", k=2),
-                in_=xg[:, :, 0:3:2, :, 1:3].rearrange("p u k c e -> p u c k e"),
-            )
+            for copy, u in ((nc.scalar.copy, 0), (nc.vector.tensor_copy, 1)):
+                copy(
+                    out=xg[:, u, 1, :, :].rearrange("p c (k e) -> p c k e", k=2),
+                    in_=xg[:, u, 0:3:2, :, 1:3].rearrange("p k c e -> p c k e"),
+                )
 
         def quantise_g(it):
             c0 = 2 * it * CO

@@ -20,9 +20,9 @@ PASSES = 32
 UNITS = 34
 XW = W_IN // 2
 GW = W_OUT // 2
-G_CUTS = [0, 2, 4, 8, 12, 16, 20, 24, 28, 32]
-N_CHUNKS = 9
-X_CUTS = [0, 4, 8, 12, 16, 20, 24, 28, 32, 34]
+G_CUTS = list(range(0, PASSES + 1, 4))
+N_CHUNKS = 8
+X_CUTS = [0] + list(range(6, UNITS + 1, 4))
 AHEAD = 4
 ROUNDS = PASSES // 2
 TAPW = 3 * CI
@@ -83,7 +83,7 @@ def tile_model_pa_kernel(tc, x, g, out):
             return 0 <= it < ROUNDS
 
         def has_x(it):
-            return -2 <= it < ROUNDS - 1
+            return -1 <= it < ROUNDS
 
         def stage_of(it):
             return stage.setdefault(it, {})
@@ -102,8 +102,8 @@ def tile_model_pa_kernel(tc, x, g, out):
             )
 
         def sort_x(it):
-            c = chunk_of(X_CUTS, 2 * it + 4)
-            u0 = 2 * it + 4 - X_CUTS[c]
+            c = chunk_of(X_CUTS, 2 * it + 2)
+            u0 = 2 * it + 2 - X_CUTS[c]
             xr = rl_pool.tile([P, 2, 3, P], F32, name="xr")
             stage_of(it)["xr"] = xr
             rows = xn_tiles[c][:].bitcast(F32)[:, :, :, u0 * XW : (u0 + 2) * XW].rearrange("p n a (u k) -> p u (n a) k", u=2, k=XW)
@@ -174,7 +174,7 @@ def tile_model_pa_kernel(tc, x, g, out):
 
         def quantise_x(it):
             flat = stage_of(it)["xg"][:].rearrange("p u k c t -> p (u k c t)")
-            c0 = (2 * it + 4) * TAPW
+            c0 = (2 * it + 2) * TAPW
             nc.vector.quantize_mx(
                 out=x_codes[:, c0 : c0 + 512].bitcast(FP8X4),
                 scales=x_scales[:, c0 : c0 + 512],
@@ -211,35 +211,33 @@ def tile_model_pa_kernel(tc, x, g, out):
 
         for c in range(AHEAD):
             load_chunk(c)
-        for it in range(-3, ROUNDS + 1):
+        for it in range(-2, ROUNDS + 1):
+            if has_x(it - 1):
+                middle_tap(it - 1)
             if has_g(it - 1):
                 quantise_g(it - 1)
             if has_x(it - 1):
-                middle_tap(it - 1)
-            if has_x(it - 1) and it <= 0:
-                quantise_x(it - 1)
-            if has_g(it + 1):
-                sort_g(it + 1)
-            if has_x(it - 1) and it > 0:
                 quantise_x(it - 1)
             if has_x(it + 1):
                 sort_x(it + 1)
+            if has_g(it + 1):
+                sort_g(it + 1)
             done = 2 * (it + 1) + 2
             if done in G_CUTS[1:] and G_CUTS.index(done) - 1 + AHEAD < N_CHUNKS:
                 load_chunk(G_CUTS.index(done) - 1 + AHEAD)
-            if has_g(it):
-                transpose_g(it)
             if has_x(it):
                 transpose_x(it)
+            if has_g(it):
+                transpose_g(it)
             if it == ROUNDS:
                 last = [tp_pool.tile([P, 512], F32, name="xb%d" % h) for h in range(2)]
                 last_tap(0, 0, 8)
             if has_g(it - 1):
                 multiply(it - 1)
-            if has_g(it):
-                copy_g(it)
             if has_x(it):
                 copy_x(it)
+            if has_g(it):
+                copy_g(it)
 
         res = [keep.tile([P, CI, 9], F32, name="res%d" % h) for h in range(2)]
 

@@ -20,10 +20,10 @@ PASSES = 32
 UNITS = 34
 XW = W_IN // 2
 GW = W_OUT // 2
-G_CUTS = list(range(0, PASSES + 1, 4))
-N_CHUNKS = 8
-X_CUTS = [0] + list(range(6, UNITS + 1, 4))
-AHEAD = 4
+G_SETS = [(0, 4), (4, 8)] + [(8 * q, 8 * q + 6) for q in range(1, 4)]
+X_SETS = [(0, 6)] + [(u, u + 4) for u in range(6, UNITS, 4)]
+V_SETS = [(8 * q + 6, 8 * q + 8) for q in range(1, 4)]
+BUFS = {"x": 3, "g": 3, "v": 2}
 ROUNDS = PASSES // 2
 TAPW = 3 * CI
 
@@ -34,7 +34,10 @@ def tile_model_pa_kernel(tc, x, g, out):
     nc = tc.nc
     with ExitStack() as ctx:
         keep = ctx.enter_context(tc.tile_pool(name="keep", bufs=1))
-        gn_pool = ctx.enter_context(tc.tile_pool(name="gn", bufs=AHEAD))
+        xn_pool = ctx.enter_context(tc.tile_pool(name="xnp", bufs=BUFS["x"]))
+        gn_pool = ctx.enter_context(tc.tile_pool(name="gnp", bufs=BUFS["g"]))
+        vn_pool = ctx.enter_context(tc.tile_pool(name="vnp", bufs=BUFS["v"]))
+        v_pool = ctx.enter_context(tc.tile_pool(name="vp", bufs=2))
         rl_pool = ctx.enter_context(tc.tile_pool(name="rl", bufs=2))
         gr_pool = ctx.enter_context(tc.tile_pool(name="grp", bufs=3))
         acc_pool = ctx.enter_context(tc.psum_pool(name="acc", bufs=1))
@@ -50,23 +53,23 @@ def tile_model_pa_kernel(tc, x, g, out):
         x_scales = keep.tile([P, UNITS * TAPW], U8, name="x_scales", align_bytes=64)
         acc = [[acc_pool.tile([P, 512], F32, name="acc%d%d" % (h, s)) for s in range(2)] for h in range(2)]
 
-        gn_tiles = {}
-        xn_tiles = {}
+        sets = {"x": X_SETS, "g": G_SETS, "v": V_SETS}
+        tiles = {}
+        done = {"x": 0, "g": 0, "v": 0}
         stage = {}
 
-        def load_chunk(c):
-            u0, u1 = X_CUTS[c], X_CUTS[c + 1]
+        def load_x(u0, u1):
             run = (u1 - u0) * W_IN
-            xn = gn_pool.tile([P, N_IMG, 2, (run + 15) // 16 * 16], BF16, name="xn")
-            xn_tiles[c] = xn
+            xn = xn_pool.tile([P, N_IMG, 2, (run + 15) // 16 * 16], BF16, name="xn")
             for a in range(2):
                 nc.sync.dma_start(
                     out=xn[:, :, a, 0:run],
                     in_=x[:, :, HALF * a + u0 : HALF * a + u1, :].rearrange("n c h w -> c n (h w)"),
                 )
-            r0, r1 = G_CUTS[c], G_CUTS[c + 1]
+            return xn
+
+        def load_g(r0, r1):
             gn = gn_pool.tile([P, 2, N_IMG, 2, (r1 - r0) * W_OUT], BF16, name="gn")
-            gn_tiles[c] = gn
             for h in range(2):
                 for a in range(2):
                     nc.sync.dma_start(
@@ -75,23 +78,56 @@ def tile_model_pa_kernel(tc, x, g, out):
                             "n c h w -> c n (h w)"
                         ),
                     )
+            return gn
 
-        def chunk_of(cuts, first):
-            return max(c for c in range(N_CHUNKS) if cuts[c] <= first)
+        def load_v(r0, r1):
+            vn = vn_pool.tile([P, CO // 32, 2, (r1 - r0) * W_OUT], BF16, name="vn")
+            for n in range(N_IMG):
+                for a in range(2):
+                    nc.sync.dma_start(
+                        out=vn[32 * n : 32 * n + 32, :, a, :],
+                        in_=g[n, :, HALF * a + r0 : HALF * a + r1, :].rearrange("(k c) h w -> c k (h w)", c=32),
+                    )
+            return vn
 
-        def has_g(it):
-            return 0 <= it < ROUNDS
+        load = {"x": load_x, "g": load_g, "v": load_v}
+        waiting = sorted(
+            [(lo - 4, 0, "x", i) for i, (lo, hi) in enumerate(X_SETS)]
+            + [(lo, 1, "g", i) for i, (lo, hi) in enumerate(G_SETS)]
+            + [(lo - 4, 2, "v", i) for i, (lo, hi) in enumerate(V_SETS)]
+        )
+
+        def issue_loads():
+            while waiting:
+                first, rank, kind, i = waiting[0]
+                if i >= BUFS[kind] and done[kind] < sets[kind][i - BUFS[kind]][1]:
+                    return
+                waiting.remove(waiting[0])
+                tiles[kind, i] = load[kind](*sets[kind][i])
+
+        def find(kind, first):
+            i = max(i for i, (lo, hi) in enumerate(sets[kind]) if lo <= first)
+            return tiles[kind, i], first - sets[kind][i][0]
 
         def has_x(it):
             return -1 <= it < ROUNDS
+
+        def exists_g(it):
+            return 0 <= it < ROUNDS
+
+        def on_vector(it):
+            return (2 * it, 2 * it + 2) in V_SETS
+
+        def has_g(it):
+            return exists_g(it) and not on_vector(it)
 
         def stage_of(it):
             return stage.setdefault(it, {})
 
         def sort_g(it):
-            c = chunk_of(G_CUTS, 2 * it)
-            l0 = 2 * it - G_CUTS[c]
-            gn_w = gn_tiles[c][:].bitcast(F32)
+            gn, l0 = find("g", 2 * it)
+            gn_w = gn[:].bitcast(F32)
+            done["g"] = 2 * it + 2
             gr = rl_pool.tile([P, 2, 2, 2, P], F32, name="gr")
             stage_of(it)["gr"] = gr
             nc.vector.tensor_copy(
@@ -102,11 +138,11 @@ def tile_model_pa_kernel(tc, x, g, out):
             )
 
         def sort_x(it):
-            c = chunk_of(X_CUTS, 2 * it + 2)
-            u0 = 2 * it + 2 - X_CUTS[c]
+            xn, u0 = find("x", 2 * it + 2)
+            done["x"] = 2 * it + 4
             xr = rl_pool.tile([P, 2, 3, P], F32, name="xr")
             stage_of(it)["xr"] = xr
-            rows = xn_tiles[c][:].bitcast(F32)[:, :, :, u0 * XW : (u0 + 2) * XW].rearrange("p n a (u k) -> p u (n a) k", u=2, k=XW)
+            rows = xn[:].bitcast(F32)[:, :, :, u0 * XW : (u0 + 2) * XW].rearrange("p n a (u k) -> p u (n a) k", u=2, k=XW)
             nc.vector.tensor_copy(
                 out=xr[:, :, 0:2, :].rearrange("p u w (x b) -> p u w x b", b=16),
                 in_=rows[:, :, :, 0:32].rearrange("p u x (b w) -> p u w x b", w=2),
@@ -136,13 +172,40 @@ def tile_model_pa_kernel(tc, x, g, out):
                 for w in range(3):
                     nc.tensor.transpose(xb[:, w * P : (w + 1) * P], st["xr"][:, lu, w, :], ident[:])
 
-        def copy_g(it):
+        def grouped(it):
             st = stage_of(it)
-            gg = gr_pool.tile([P, 2, CO, 4], BF16, name="gg", align_bytes=64)
-            st["gg"] = gg
-            gg_w = gg[:].bitcast(F32)
+            if "gg" not in st:
+                gg = gr_pool.tile([P, 2, CO, 4], BF16, name="gg", align_bytes=64)
+                st["gg"] = gg
+            return st["gg"][:].bitcast(F32)
+
+        def copy_g(it):
             for li in range(2):
-                nc.scalar.copy(out=gg_w[:, li], in_=st["gb"][li][:].rearrange("p (w c) -> p c w", w=2))
+                nc.scalar.copy(
+                    out=grouped(it)[:, li], in_=stage_of(it)["gb"][li][:].rearrange("p (w c) -> p c w", w=2)
+                )
+
+        def sort_v(r):
+            vn, l0 = find("v", r)
+            done["v"] = r + 1
+            ds = v_pool.tile([P, 2, CO // 16, 16], F32, name="ds", align_bytes=64)
+            stage_of(r // 2)["ds", r] = ds
+            nc.scalar.copy(
+                out=ds[:],
+                in_=vn[:].bitcast(F32)[:, :, :, l0 * GW : (l0 + 1) * GW].rearrange("p k a (b w) -> p w (k a) b", w=2),
+            )
+
+        def turn_v(r):
+            st = stage_of(r // 2)
+            dt = v_pool.tile([P, 2 * CO], F32, name="dt", align_bytes=64)
+            st["dt", r] = dt
+            nc.vector.transpose(out=dt[:], in_=st["ds", r][:].rearrange("p w x b -> p (w x b)"))
+
+        def merge_v(r):
+            nc.scalar.copy(
+                out=grouped(r // 2)[:, r % 2],
+                in_=stage_of(r // 2)["dt", r][:].rearrange("p (w c) -> p c w", w=2),
+            )
 
         def copy_x(it):
             st = stage_of(it)
@@ -209,12 +272,11 @@ def tile_model_pa_kernel(tc, x, g, out):
             for r in range(r0, r1):
                 mx_pass(last[h][:, 0:P], r, h, 1024, P)
 
-        for c in range(AHEAD):
-            load_chunk(c)
+        issue_loads()
         for it in range(-2, ROUNDS + 1):
             if has_x(it - 1):
                 middle_tap(it - 1)
-            if has_g(it - 1):
+            if exists_g(it - 1):
                 quantise_g(it - 1)
             if has_x(it - 1):
                 quantise_x(it - 1)
@@ -222,9 +284,11 @@ def tile_model_pa_kernel(tc, x, g, out):
                 sort_x(it + 1)
             if has_g(it + 1):
                 sort_g(it + 1)
-            done = 2 * (it + 1) + 2
-            if done in G_CUTS[1:] and G_CUTS.index(done) - 1 + AHEAD < N_CHUNKS:
-                load_chunk(G_CUTS.index(done) - 1 + AHEAD)
+            if on_vector(it + 2):
+                turn_v(2 * (it + 2))
+            if on_vector(it + 1):
+                turn_v(2 * (it + 1) + 1)
+            issue_loads()
             if has_x(it):
                 transpose_x(it)
             if has_g(it):
@@ -232,12 +296,20 @@ def tile_model_pa_kernel(tc, x, g, out):
             if it == ROUNDS:
                 last = [tp_pool.tile([P, 512], F32, name="xb%d" % h) for h in range(2)]
                 last_tap(0, 0, 8)
-            if has_g(it - 1):
+            if exists_g(it - 1):
                 multiply(it - 1)
+            if on_vector(it):
+                merge_v(2 * it)
             if has_x(it):
                 copy_x(it)
+            if on_vector(it):
+                merge_v(2 * it + 1)
             if has_g(it):
                 copy_g(it)
+            if on_vector(it + 3):
+                sort_v(2 * (it + 3))
+            if on_vector(it + 2):
+                sort_v(2 * (it + 2) + 1)
 
         res = [keep.tile([P, CI, 9], F32, name="res%d" % h) for h in range(2)]
 

@@ -21,7 +21,7 @@ UNITS = 34
 XW = W_IN // 2
 GW = W_OUT // 2
 G_SETS = [(0, 4), (4, 8)] + [(8 * q, 8 * q + 6) for q in range(1, 4)]
-X_SETS = [(0, 6)] + [(u, u + 4) for u in range(6, UNITS, 4)]
+X_SETS = [(u, min(u + 4, UNITS)) for u in range(0, UNITS, 4)]
 V_SETS = [(8 * q + 6, 8 * q + 8) for q in range(1, 4)]
 BUFS = {"x": 3, "g": 3, "v": 2}
 ROUNDS = PASSES // 2
@@ -44,6 +44,8 @@ def tile_model_pa_kernel(tc, x, g, out):
         tp_pool = ctx.enter_context(tc.psum_pool(name="tp", bufs=1))
         ctx.enter_context(tc.manual_schedule())
 
+        blank = keep.tile([P, 512], BF16, name="blank")
+        nc.vector.memset(blank[:], 0.0)
         ident = keep.tile([P, P], F32, name="ident")
         make_identity(nc, ident[:])
 
@@ -92,8 +94,8 @@ def tile_model_pa_kernel(tc, x, g, out):
 
         load = {"x": load_x, "g": load_g, "v": load_v}
         waiting = sorted(
-            [(lo - 4, 0, "x", i) for i, (lo, hi) in enumerate(X_SETS)]
-            + [(lo, 1, "g", i) for i, (lo, hi) in enumerate(G_SETS)]
+            [(lo - 2, 1, "x", i) for i, (lo, hi) in enumerate(X_SETS)]
+            + [(lo, 0, "g", i) for i, (lo, hi) in enumerate(G_SETS)]
             + [(lo - 4, 2, "v", i) for i, (lo, hi) in enumerate(V_SETS)]
         )
 
@@ -272,7 +274,12 @@ def tile_model_pa_kernel(tc, x, g, out):
             for r in range(r0, r1):
                 mx_pass(last[h][:, 0:P], r, h, 1024, P)
 
+        def keep_warm(passes):
+            for i in range(passes):
+                nc.tensor.matmul(acc[0][0][:], lhsT=blank[:, 0:P], rhs=blank[:], start=True, stop=True)
+
         issue_loads()
+        keep_warm(8)
         for it in range(-2, ROUNDS + 1):
             if has_x(it - 1):
                 middle_tap(it - 1)
@@ -291,8 +298,12 @@ def tile_model_pa_kernel(tc, x, g, out):
             issue_loads()
             if has_x(it):
                 transpose_x(it)
+                if it < 1:
+                    keep_warm(4)
             if has_g(it):
                 transpose_g(it)
+                if it < 1:
+                    keep_warm(4)
             if it == ROUNDS:
                 last = [tp_pool.tile([P, 512], F32, name="xb%d" % h) for h in range(2)]
                 last_tap(0, 0, 8)
@@ -325,8 +336,8 @@ def tile_model_pa_kernel(tc, x, g, out):
         last_tap(0, 8, PASSES)
         last_tap(1, 0, PASSES)
         for h in range(2):
-            for c0 in range(0, CI, CI // 2):
-                cs = slice(c0, c0 + CI // 2)
+            for c0 in range(0, CI, CI // 4):
+                cs = slice(c0, c0 + CI // 4)
                 leave(h, res[h][:, cs, 8:9], last[h][:, cs].rearrange("p (c o) -> p c o", o=1))
                 nc.sync.dma_start(
                     out=out[h * P : (h + 1) * P, cs].rearrange("o c kh kw -> o (c kh kw)"),

@@ -20,9 +20,11 @@ PASSES = 32
 UNITS = 34
 XW = W_IN // 2
 GW = W_OUT // 2
-G_SETS = [(0, 4), (4, 8)] + [(8 * q, 8 * q + 6) for q in range(1, 4)]
 X_SETS = [(u, min(u + 4, UNITS)) for u in range(0, UNITS, 4)]
-V_SETS = [(8 * q + 6, 8 * q + 8) for q in range(1, 4)]
+V_SETS = [(2 * k, 2 * k + 2) for k in range(5, PASSES // 2, 3)]
+G_SETS = [(r, min(r + 4, V_SETS[0][0])) for r in range(0, V_SETS[0][0], 4)] + [
+    (hi, min(hi + 4, PASSES)) for lo, hi in V_SETS
+]
 BUFS = {"x": 3, "g": 3, "v": 2}
 ROUNDS = PASSES // 2
 TAPW = 3 * CI

@@ -21,9 +21,9 @@ UNITS = 34
 XW = W_IN // 2
 GW = W_OUT // 2
 X_SETS = [(u, min(u + 4, UNITS)) for u in range(0, UNITS, 4)]
-V_SETS = [(2 * k, 2 * k + 2) for k in range(5, PASSES // 2, 3)]
+V_SETS = [(2 * k, 2 * k + 2) for k in range(9, PASSES // 2, 3)]
 G_SETS = [(r, min(r + 4, V_SETS[0][0])) for r in range(0, V_SETS[0][0], 4)] + [
-    (hi, min(hi + 4, PASSES)) for lo, hi in V_SETS
+    (hi, hi + 4) for lo, hi in V_SETS if hi < PASSES
 ]
 BUFS = {"x": 3, "g": 3, "v": 2}
 ROUNDS = PASSES // 2
@@ -285,13 +285,15 @@ def tile_model_pa_kernel(tc, x, g, out):
         for it in range(-2, ROUNDS + 1):
             if has_x(it - 1):
                 middle_tap(it - 1)
+            if it == 0:
+                sort_g(0)
             if exists_g(it - 1):
                 quantise_g(it - 1)
             if has_x(it - 1):
                 quantise_x(it - 1)
             if has_x(it + 1):
                 sort_x(it + 1)
-            if has_g(it + 1):
+            if has_g(it + 1) and it >= 0:
                 sort_g(it + 1)
             if on_vector(it + 2):
                 turn_v(2 * (it + 2))

@@ -21,7 +21,7 @@ UNITS = 34
 XW = W_IN // 2
 GW = W_OUT // 2
 X_SETS = [(u, min(u + 4, UNITS)) for u in range(0, UNITS, 4)]
-V_SETS = [(2 * k, 2 * k + 2) for k in range(9, PASSES // 2, 3)]
+V_SETS = [(2 * k, 2 * k + 2) for k in range(6, PASSES // 2, 3)]
 G_SETS = [(r, min(r + 4, V_SETS[0][0])) for r in range(0, V_SETS[0][0], 4)] + [
     (hi, hi + 4) for lo, hi in V_SETS if hi < PASSES
 ]
@@ -189,12 +189,12 @@ def tile_model_pa_kernel(tc, x, g, out):
                     out=grouped(it)[:, li], in_=stage_of(it)["gb"][li][:].rearrange("p (w c) -> p c w", w=2)
                 )
 
-        def sort_v(r):
+        def sort_v(r, copy):
             vn, l0 = find("v", r)
             done["v"] = r + 1
             ds = v_pool.tile([P, 2, CO // 16, 16], F32, name="ds", align_bytes=64)
             stage_of(r // 2)["ds", r] = ds
-            nc.scalar.copy(
+            copy(
                 out=ds[:],
                 in_=vn[:].bitcast(F32)[:, :, :, l0 * GW : (l0 + 1) * GW].rearrange("p k a (b w) -> p w (k a) b", w=2),
             )
@@ -225,7 +225,8 @@ def tile_model_pa_kernel(tc, x, g, out):
 
         def middle_tap(it):
             xg = stage_of(it)["xg"]
-            for copy, u in ((nc.scalar.copy, 0), (nc.vector.tensor_copy, 1)):
+            second = nc.scalar.copy if on_vector(it + 3) else nc.vector.tensor_copy
+            for copy, u in ((nc.scalar.copy, 0), (second, 1)):
                 copy(
                     out=xg[:, u, 1, :, :].rearrange("p c (k e) -> p c k e", k=2),
                     in_=xg[:, u, 0:3:2, :, 1:3].rearrange("p k c e -> p c k e"),
@@ -295,6 +296,8 @@ def tile_model_pa_kernel(tc, x, g, out):
                 sort_x(it + 1)
             if has_g(it + 1) and it >= 0:
                 sort_g(it + 1)
+            if on_vector(it + 3):
+                sort_v(2 * (it + 3), nc.vector.tensor_copy)
             if on_vector(it + 2):
                 turn_v(2 * (it + 2))
             if on_vector(it + 1):
@@ -321,10 +324,8 @@ def tile_model_pa_kernel(tc, x, g, out):
                 merge_v(2 * it + 1)
             if has_g(it):
                 copy_g(it)
-            if on_vector(it + 3):
-                sort_v(2 * (it + 3))
             if on_vector(it + 2):
-                sort_v(2 * (it + 2) + 1)
+                sort_v(2 * (it + 2) + 1, nc.scalar.copy)
 
         res = [keep.tile([P, CI, 9], F32, name="res%d" % h) for h in range(2)]
 

@@ -27,6 +27,8 @@ G_SETS = [(r, min(r + 4, V_SETS[0][0])) for r in range(0, V_SETS[0][0], 4)] + [
 ]
 BUFS = {"x": 3, "g": 3, "v": 2}
 ROUNDS = PASSES // 2
+GROUPS = 2
+CG = CI // GROUPS
 TAPW = 3 * CI
 
 FLOPS = 2 * CO * CI * 9 * N_IMG * W_OUT * W_OUT
@@ -213,23 +215,33 @@ def tile_model_pa_kernel(tc, x, g, out):
 
         def copy_x(it):
             st = stage_of(it)
-            xg = gr_pool.tile([P, 2, 3, CI, 4], BF16, name="xg", align_bytes=64)
+            xg = gr_pool.tile([P, 2, GROUPS, 3, CG, 4], BF16, name="xg", align_bytes=64)
             st["xg"] = xg
             xg_w = xg[:].bitcast(F32)
             for lu in range(2):
                 for k in range(2):
                     nc.scalar.copy(
-                        out=xg_w[:, lu, 2 * k],
-                        in_=st["xb"][lu][:, k * P : (k + 2) * P].rearrange("p (w c) -> p c w", w=2),
+                        out=xg_w[:, lu, :, 2 * k],
+                        in_=st["xb"][lu][:, k * P : (k + 2) * P].rearrange("p (w g c) -> p g c w", w=2, g=GROUPS),
                     )
 
         def middle_tap(it):
             xg = stage_of(it)["xg"]
-            second = nc.scalar.copy if on_vector(it + 3) else nc.vector.tensor_copy
-            for copy, u in ((nc.scalar.copy, 0), (second, 1)):
-                copy(
-                    out=xg[:, u, 1, :, :].rearrange("p c (k e) -> p c k e", k=2),
-                    in_=xg[:, u, 0:3:2, :, 1:3].rearrange("p k c e -> p c k e"),
+            for g in range(GROUPS):
+                nc.scalar.copy(
+                    out=xg[:, 0, g, 1, :, :].rearrange("p c (k e) -> p c k e", k=2),
+                    in_=xg[:, 0, g, 0:3:2, :, 1:3].rearrange("p k c e -> p c k e"),
+                )
+            if on_vector(it + 3):
+                for g in range(GROUPS):
+                    nc.scalar.copy(
+                        out=xg[:, 1, g, 1, :, :].rearrange("p c (k e) -> p c k e", k=2),
+                        in_=xg[:, 1, g, 0:3:2, :, 1:3].rearrange("p k c e -> p c k e"),
+                    )
+            else:
+                nc.vector.tensor_copy(
+                    out=xg[:, 1, :, 1, :, :].rearrange("p g c (k e) -> p g c k e", k=2),
+                    in_=xg[:, 1, :, 0:3:2, :, 1:3].rearrange("p g k c e -> p g c k e"),
                 )
 
         def quantise_g(it):
@@ -241,7 +253,7 @@ def tile_model_pa_kernel(tc, x, g, out):
             )
 
         def quantise_x(it):
-            flat = stage_of(it)["xg"][:].rearrange("p u k c t -> p (u k c t)")
+            flat = stage_of(it)["xg"][:].rearrange("p u g k c t -> p (u g k c t)")
             c0 = (2 * it + 2) * TAPW
             nc.vector.quantize_mx(
                 out=x_codes[:, c0 : c0 + 512].bitcast(FP8X4),
@@ -327,24 +339,33 @@ def tile_model_pa_kernel(tc, x, g, out):
             if on_vector(it + 2):
                 sort_v(2 * (it + 2) + 1, nc.scalar.copy)
 
-        res = [keep.tile([P, CI, 9], F32, name="res%d" % h) for h in range(2)]
+        res = [keep.tile([P, GROUPS, CG, 9], F32, name="res%d" % h) for h in range(2)]
 
         def leave(h, dst, src):
-            if h == 0:
-                nc.vector.tensor_copy(out=dst, in_=src)
-            else:
-                nc.scalar.copy(out=dst, in_=src)
+            copy = nc.vector.tensor_copy if h == 0 else nc.scalar.copy
+            copy(out=dst, in_=src)
 
-        for s in range(2):
-            for h in range(2):
-                leave(h, res[h][:, :, 4 * s : 4 * s + 4], acc[h][s][:].rearrange("p (t c) -> p c t", t=4))
+        def store(h, g, c0, c1):
+            nc.sync.dma_start(
+                out=out[h * P : (h + 1) * P, CG * g + c0 : CG * g + c1].rearrange("o c kh kw -> o (c kh kw)"),
+                in_=res[h][:, g, c0:c1].rearrange("p c t -> p (c t)"),
+            )
+
+        for h in range(2):
+            leave(h, res[h][:, 0, :, 0:3], acc[h][0][:, 0 : 3 * CG].rearrange("p (t c) -> p c t", t=3))
+            leave(h, res[h][:, 0, :, 3:5], acc[h][0][:, 6 * CG : 8 * CG].rearrange("p (t c) -> p c t", t=2))
+            leave(h, res[h][:, 0, :, 5:6], acc[h][1][:, 0:CG].rearrange("p (t c) -> p c t", t=1))
+            leave(h, res[h][:, 0, :, 6:9], acc[h][1][:, 4 * CG : 7 * CG].rearrange("p (t c) -> p c t", t=3))
+            store(h, 0, 0, CG)
+        for h in range(2):
+            leave(h, res[h][:, 1, :, 0:3], acc[h][0][:, 3 * CG : 6 * CG].rearrange("p (t c) -> p c t", t=3))
+            leave(h, res[h][:, 1, :, 3:6], acc[h][1][:, CG : 4 * CG].rearrange("p (t c) -> p c t", t=3))
+            leave(h, res[h][:, 1, :, 6:7], acc[h][1][:, 7 * CG : 8 * CG].rearrange("p (t c) -> p c t", t=1))
         last_tap(0, 8, PASSES)
         last_tap(1, 0, PASSES)
         for h in range(2):
-            for c0 in range(0, CI, CI // 4):
-                cs = slice(c0, c0 + CI // 4)
-                leave(h, res[h][:, cs, 8:9], last[h][:, cs].rearrange("p (c o) -> p c o", o=1))
-                nc.sync.dma_start(
-                    out=out[h * P : (h + 1) * P, cs].rearrange("o c kh kw -> o (c kh kw)"),
-                    in_=res[h][:, cs].rearrange("p c t -> p (c t)"),
-                )
+            left = last[h][:, 0:P].rearrange("p (t c) -> p t c", t=2)
+            for c0 in range(0, CG, CG // 2):
+                c1 = c0 + CG // 2
+                leave(h, res[h][:, 1, c0:c1, 7:9], left[:, :, c0:c1].rearrange("p t c -> p c t"))
+                store(h, 1, c0, c1)

@@ -20,16 +20,18 @@ PASSES = 32
 UNITS = 34
 XW = W_IN // 2
 GW = W_OUT // 2
-X_SETS = [(u, min(u + 4, UNITS)) for u in range(0, UNITS, 4)]
-V_SETS = [(2 * k, 2 * k + 2) for k in range(6, PASSES // 2, 3)]
-G_SETS = [(r, min(r + 4, V_SETS[0][0])) for r in range(0, V_SETS[0][0], 4)] + [
-    (hi, hi + 4) for lo, hi in V_SETS if hi < PASSES
-]
-BUFS = {"x": 3, "g": 3, "v": 2}
 ROUNDS = PASSES // 2
+STAGES = UNITS // 2
 GROUPS = 2
 CG = CI // GROUPS
 TAPW = 3 * CI
+X_SETS = [(u, min(u + 4, UNITS)) for u in range(0, UNITS, 4)]
+SETS = [(0, 4, "g"), (4, 8, "g"), (8, 12, "g"), (12, 14, "g"), (14, 16, "v"), (16, 18, "g"), (18, 20, "v"), (20, 22, "g"), (22, 24, "v"), (24, 26, "g"), (26, 28, "v"), (28, 30, "g"), (30, 32, "v")]
+G_SETS = [s[:2] for s in SETS if s[2] == "g"]
+V_SETS = [s[:2] for s in SETS if s[2] == "v"]
+T_PAIRS = [r // 2 for lo, hi in G_SETS for r in range(lo, hi, 2)]
+V_ROWS = [r for lo, hi in V_SETS for r in range(lo, hi)]
+BUFS = {"x": 3, "g": 3, "v": 3}
 
 FLOPS = 2 * CO * CI * 9 * N_IMG * W_OUT * W_OUT
 
@@ -62,7 +64,9 @@ def tile_model_pa_kernel(tc, x, g, out):
         sets = {"x": X_SETS, "g": G_SETS, "v": V_SETS}
         tiles = {}
         done = {"x": 0, "g": 0, "v": 0}
-        stage = {}
+        xs = {}
+        gs = {}
+        vs = {}
 
         def load_x(u0, u1):
             run = (u1 - u0) * W_IN
@@ -88,7 +92,7 @@ def tile_model_pa_kernel(tc, x, g, out):
 
         def load_v(r0, r1):
             vn = vn_pool.tile([P, CO // 32, 2, (r1 - r0) * W_OUT], BF16, name="vn")
-            for n in range(N_IMG):
+            for n in (0, 2, 1, 3):
                 for a in range(2):
                     nc.sync.dma_start(
                         out=vn[32 * n : 32 * n + 32, :, a, :],
@@ -97,15 +101,11 @@ def tile_model_pa_kernel(tc, x, g, out):
             return vn
 
         load = {"x": load_x, "g": load_g, "v": load_v}
-        waiting = sorted(
-            [(lo - 2, 1, "x", i) for i, (lo, hi) in enumerate(X_SETS)]
-            + [(lo, 0, "g", i) for i, (lo, hi) in enumerate(G_SETS)]
-            + [(lo - 4, 2, "v", i) for i, (lo, hi) in enumerate(V_SETS)]
-        )
+        waiting = [("x", 0), ("g", 0), ("x", 1), ("g", 1), ("x", 2), ("g", 2), ("x", 3), ("v", 0), ("g", 3), ("x", 4), ("v", 1), ("g", 4), ("x", 5), ("v", 2), ("g", 5), ("x", 6), ("v", 3), ("g", 6), ("x", 7), ("v", 4), ("g", 7), ("x", 8)]
 
         def issue_loads():
             while waiting:
-                first, rank, kind, i = waiting[0]
+                kind, i = waiting[0]
                 if i >= BUFS[kind] and done[kind] < sets[kind][i - BUFS[kind]][1]:
                     return
                 waiting.remove(waiting[0])
@@ -115,156 +115,137 @@ def tile_model_pa_kernel(tc, x, g, out):
             i = max(i for i, (lo, hi) in enumerate(sets[kind]) if lo <= first)
             return tiles[kind, i], first - sets[kind][i][0]
 
-        def has_x(it):
-            return -1 <= it < ROUNDS
-
-        def exists_g(it):
-            return 0 <= it < ROUNDS
-
-        def on_vector(it):
-            return (2 * it, 2 * it + 2) in V_SETS
-
-        def has_g(it):
-            return exists_g(it) and not on_vector(it)
-
-        def stage_of(it):
-            return stage.setdefault(it, {})
-
-        def sort_g(it):
-            gn, l0 = find("g", 2 * it)
-            gn_w = gn[:].bitcast(F32)
-            done["g"] = 2 * it + 2
-            gr = rl_pool.tile([P, 2, 2, 2, P], F32, name="gr")
-            stage_of(it)["gr"] = gr
-            nc.vector.tensor_copy(
-                out=gr[:].rearrange("p i w h (x b) -> p i w (h x) b", b=16),
-                in_=gn_w[:, :, :, :, l0 * GW : (l0 + 2) * GW].rearrange(
-                    "p h n a (i b w) -> p i w (h n a) b", i=2, b=16, w=2
-                ),
+        def sort_x(k, stages):
+            xn, u0 = find("x", 2 * k)
+            units = 2 * stages
+            done["x"] = 2 * k + units
+            xr = rl_pool.tile([P, units, 3, P], F32, name="xr%d" % units)
+            for i in range(stages):
+                xs[k + i] = {"xr": xr, "lu": 2 * i}
+            rows = xn[:].bitcast(F32)[:, :, :, u0 * XW : (u0 + units) * XW].rearrange(
+                "p n a (u k) -> p u (n a) k", u=units, k=XW
             )
-
-        def sort_x(it):
-            xn, u0 = find("x", 2 * it + 2)
-            done["x"] = 2 * it + 4
-            xr = rl_pool.tile([P, 2, 3, P], F32, name="xr")
-            stage_of(it)["xr"] = xr
-            rows = xn[:].bitcast(F32)[:, :, :, u0 * XW : (u0 + 2) * XW].rearrange("p n a (u k) -> p u (n a) k", u=2, k=XW)
             nc.vector.tensor_copy(
                 out=xr[:, :, 0:2, :].rearrange("p u w (x b) -> p u w x b", b=16),
                 in_=rows[:, :, :, 0:32].rearrange("p u x (b w) -> p u w x b", w=2),
             )
-            nc.vector.tensor_copy(
+            (nc.scalar.copy if k in range(5, 17, 2) else nc.vector.tensor_copy)(
                 out=xr[:, :, 2, :].rearrange("p u (x b) -> p u x b", b=16),
                 in_=rows[:, :, :, 2:33:2],
             )
 
-        def transpose_g(it):
-            st = stage_of(it)
-            st["gb"] = []
-            for li in range(2):
-                gb = tp_pool.tile([P, 512], F32, name="gb%d" % li)
-                st["gb"].append(gb)
-                for w in range(2):
-                    for h in range(2):
-                        k = 2 * w + h
-                        nc.tensor.transpose(gb[:, k * P : (k + 1) * P], st["gr"][:, li, w, h, :], ident[:])
-
-        def transpose_x(it):
-            st = stage_of(it)
-            st["xb"] = []
+        def transpose_x(k, bank="xb%d"):
+            xs[k]["xb"] = []
             for lu in range(2):
-                xb = tp_pool.tile([P, 512], F32, name="xb%d" % lu)
-                st["xb"].append(xb)
+                xb = tp_pool.tile([P, 512], F32, name=bank % lu)
+                xs[k]["xb"].append(xb)
                 for w in range(3):
-                    nc.tensor.transpose(xb[:, w * P : (w + 1) * P], st["xr"][:, lu, w, :], ident[:])
+                    nc.tensor.transpose(xb[:, w * P : (w + 1) * P], xs[k]["xr"][:, xs[k]["lu"] + lu, w, :], ident[:])
 
-        def grouped(it):
-            st = stage_of(it)
-            if "gg" not in st:
-                gg = gr_pool.tile([P, 2, CO, 4], BF16, name="gg", align_bytes=64)
-                st["gg"] = gg
-            return st["gg"][:].bitcast(F32)
+        def copy_x(k, unit=None, copy=nc.scalar.copy):
+            if "xg" not in xs[k]:
+                xg = gr_pool.tile([P, 2, GROUPS, 3, CG, 4], BF16, name="xg", align_bytes=64)
+                xs[k]["xg"] = xg
+            xg_w = xs[k]["xg"][:].bitcast(F32)
+            for lu in range(2) if unit is None else (unit,):
+                for j in range(2):
+                    copy(
+                        out=xg_w[:, lu, :, 2 * j],
+                        in_=xs[k]["xb"][lu][:, j * P : (j + 2) * P].rearrange("p (w g c) -> p g c w", w=2, g=GROUPS),
+                    )
 
-        def copy_g(it):
-            for li in range(2):
-                nc.scalar.copy(
-                    out=grouped(it)[:, li], in_=stage_of(it)["gb"][li][:].rearrange("p (w c) -> p c w", w=2)
+        def middle_tap(k, units, on_scalar=False):
+            flat = xs[k]["xg"][:].rearrange("p u g k c t -> p (u g) k c t")
+            blocks = range(GROUPS * units[0], GROUPS * (units[-1] + 1))
+            if on_scalar:
+                for v in blocks:
+                    nc.scalar.copy(
+                        out=flat[:, v, 1].rearrange("p c (k e) -> p c k e", k=2),
+                        in_=flat[:, v, 0:3:2, :, 1:3].rearrange("p k c e -> p c k e"),
+                    )
+            else:
+                bs = slice(blocks[0], blocks[-1] + 1)
+                nc.vector.tensor_copy(
+                    out=flat[:, bs, 1].rearrange("p v c (k e) -> p v c k e", k=2),
+                    in_=flat[:, bs, 0:3:2, :, 1:3].rearrange("p v k c e -> p v c k e"),
                 )
+
+        def quantise_x(k, lo, hi):
+            c0 = 2 * k * TAPW
+            nc.vector.quantize_mx(
+                out=x_codes[:, c0 + lo : c0 + hi].bitcast(FP8X4),
+                scales=x_scales[:, c0 + lo : c0 + hi],
+                in_=xs[k]["xg"][:].rearrange("p u g k c t -> p (u g k c t)")[:, 4 * lo : 4 * hi],
+            )
+
+        def quantise_stage(k):
+            quantise_x(k, 0, 512)
+            quantise_x(k, 512, 768)
+
+        def quantise_unit(k, u):
+            quantise_x(k, 384 * u, 384 * u + 256)
+            quantise_x(k, 384 * u + 256, 384 * u + 384)
+
+        def sort_g(q, li0, li1, copy, h0=0, h1=2):
+            gn, l0 = find("g", 2 * q)
+            done["g"] = 2 * q + li1
+            if q not in gs:
+                gr = rl_pool.tile([P, 2, 2, 2, P], F32, name="gr")
+                gg = gr_pool.tile([P, 2, CO, 4], BF16, name="gg", align_bytes=64)
+                gs[q] = {"gr": gr, "gg": gg}
+            copy(
+                out=gs[q]["gr"][:, li0:li1, :, h0:h1].rearrange("p i w h (x b) -> p i w (h x) b", b=16),
+                in_=gn[:].bitcast(F32)[:, h0:h1, :, :, (l0 + li0) * GW : (l0 + li1) * GW].rearrange(
+                    "p h n a (i b w) -> p i w (h n a) b", i=li1 - li0, b=16, w=2
+                ),
+            )
+
+        def transpose_g(q, li):
+            gb = tp_pool.tile([P, 512], F32, name="gb%d" % li)
+            gs[q]["gb", li] = gb
+            for w in range(2):
+                for h in range(2):
+                    k = 2 * w + h
+                    nc.tensor.transpose(gb[:, k * P : (k + 1) * P], gs[q]["gr"][:, li, w, h, :], ident[:])
+
+        def copy_g(q, li, copy):
+            copy(
+                out=gs[q]["gg"][:].bitcast(F32)[:, li],
+                in_=gs[q]["gb", li][:].rearrange("p (w c) -> p c w", w=2),
+            )
+
+        def quantise(gg, c0, width):
+            nc.vector.quantize_mx(
+                out=g_codes[:, c0 : c0 + width].bitcast(FP8X4),
+                scales=g_scales[:, c0 : c0 + width],
+                in_=gg,
+            )
+
+        def quantise_g(q):
+            quantise(gs[q]["gg"][:].rearrange("p i c t -> p (i c t)"), 2 * q * CO, 2 * CO)
 
         def sort_v(r, copy):
             vn, l0 = find("v", r)
             done["v"] = r + 1
             ds = v_pool.tile([P, 2, CO // 16, 16], F32, name="ds", align_bytes=64)
-            stage_of(r // 2)["ds", r] = ds
+            vs[r] = {"ds": ds}
             copy(
                 out=ds[:],
                 in_=vn[:].bitcast(F32)[:, :, :, l0 * GW : (l0 + 1) * GW].rearrange("p k a (b w) -> p w (k a) b", w=2),
             )
 
         def turn_v(r):
-            st = stage_of(r // 2)
             dt = v_pool.tile([P, 2 * CO], F32, name="dt", align_bytes=64)
-            st["dt", r] = dt
-            nc.vector.transpose(out=dt[:], in_=st["ds", r][:].rearrange("p w x b -> p (w x b)"))
+            vs[r]["dt"] = dt
+            nc.vector.transpose(out=dt[:], in_=vs[r]["ds"][:].rearrange("p w x b -> p (w x b)"))
 
-        def merge_v(r):
-            nc.scalar.copy(
-                out=grouped(r // 2)[:, r % 2],
-                in_=stage_of(r // 2)["dt", r][:].rearrange("p (w c) -> p c w", w=2),
-            )
+        def merge_v(r, copy):
+            gv = gr_pool.tile([P, CO, 4], BF16, name="gv", align_bytes=64)
+            vs[r]["gv"] = gv
+            copy(out=gv[:].bitcast(F32), in_=vs[r]["dt"][:].rearrange("p (w c) -> p c w", w=2))
 
-        def copy_x(it):
-            st = stage_of(it)
-            xg = gr_pool.tile([P, 2, GROUPS, 3, CG, 4], BF16, name="xg", align_bytes=64)
-            st["xg"] = xg
-            xg_w = xg[:].bitcast(F32)
-            for lu in range(2):
-                for k in range(2):
-                    nc.scalar.copy(
-                        out=xg_w[:, lu, :, 2 * k],
-                        in_=st["xb"][lu][:, k * P : (k + 2) * P].rearrange("p (w g c) -> p g c w", w=2, g=GROUPS),
-                    )
-
-        def middle_tap(it):
-            xg = stage_of(it)["xg"]
-            for g in range(GROUPS):
-                nc.scalar.copy(
-                    out=xg[:, 0, g, 1, :, :].rearrange("p c (k e) -> p c k e", k=2),
-                    in_=xg[:, 0, g, 0:3:2, :, 1:3].rearrange("p k c e -> p c k e"),
-                )
-            if on_vector(it + 3):
-                for g in range(GROUPS):
-                    nc.scalar.copy(
-                        out=xg[:, 1, g, 1, :, :].rearrange("p c (k e) -> p c k e", k=2),
-                        in_=xg[:, 1, g, 0:3:2, :, 1:3].rearrange("p k c e -> p c k e"),
-                    )
-            else:
-                nc.vector.tensor_copy(
-                    out=xg[:, 1, :, 1, :, :].rearrange("p g c (k e) -> p g c k e", k=2),
-                    in_=xg[:, 1, :, 0:3:2, :, 1:3].rearrange("p g k c e -> p g c k e"),
-                )
-
-        def quantise_g(it):
-            c0 = 2 * it * CO
-            nc.vector.quantize_mx(
-                out=g_codes[:, c0 : c0 + 2 * CO].bitcast(FP8X4),
-                scales=g_scales[:, c0 : c0 + 2 * CO],
-                in_=stage_of(it)["gg"][:].rearrange("p i c t -> p (i c t)"),
-            )
-
-        def quantise_x(it):
-            flat = stage_of(it)["xg"][:].rearrange("p u g k c t -> p (u g k c t)")
-            c0 = (2 * it + 2) * TAPW
-            nc.vector.quantize_mx(
-                out=x_codes[:, c0 : c0 + 512].bitcast(FP8X4),
-                scales=x_scales[:, c0 : c0 + 512],
-                in_=flat[:, 0:2048],
-            )
-            nc.vector.quantize_mx(
-                out=x_codes[:, c0 + 512 : c0 + 768].bitcast(FP8X4),
-                scales=x_scales[:, c0 + 512 : c0 + 768],
-                in_=flat[:, 2048:3072],
-            )
+        def quantise_v(r):
+            quantise(vs[r]["gv"][:].rearrange("p c t -> p (c t)"), r * CO, CO)
 
         def mx_pass(dst, r, h, col, width):
             gc = r * CO + h * P
@@ -279,11 +260,9 @@ def tile_model_pa_kernel(tc, x, g, out):
                 stop=(r == PASSES - 1),
             )
 
-        def multiply(rd):
-            for r in (2 * rd, 2 * rd + 1):
-                for s in range(2):
-                    for h in range(2):
-                        mx_pass(acc[h][s][:], r, h, 512 * s, 512)
+        def multiply(r, s, halves=(0, 1)):
+            for h in halves:
+                mx_pass(acc[h][s][:], r, h, 512 * s, 512)
 
         def last_tap(h, r0, r1):
             for r in range(r0, r1):
@@ -295,50 +274,77 @@ def tile_model_pa_kernel(tc, x, g, out):
 
         issue_loads()
         keep_warm(8)
-        for it in range(-2, ROUNDS + 1):
-            if has_x(it - 1):
-                middle_tap(it - 1)
-            if it == 0:
-                sort_g(0)
-            if exists_g(it - 1):
+        v_copy = nc.vector.tensor_copy
+        s_copy = nc.scalar.copy
+        both = (0, 1)
+        turn_at = {5: [14], 6: [15], 7: [18], 8: [19], 9: [22], 10: [23], 11: [26], 12: [27], 13: [30], 14: [31]}
+        sorted_by_scalar = (3, 4, 5, 6, 8, 10, 12, 14,)
+        sort_x(0, 1)
+        sort_x(1, 1)
+        issue_loads()
+        transpose_x(0)
+        keep_warm(3)
+        copy_x(0)
+        sort_g(0, 0, 2, v_copy, 0, 1)
+        middle_tap(0, (0,), True)
+        middle_tap(0, (1,))
+        sort_g(0, 0, 2, v_copy, 1, 2)
+        issue_loads()
+        transpose_x(1)
+        keep_warm(2)
+        transpose_g(0, 0)
+        transpose_g(0, 1)
+        keep_warm(2)
+        quantise_stage(0)
+        copy_x(1)
+        copy_g(0, 0, s_copy)
+        copy_g(0, 1, s_copy)
+        middle_tap(1, both)
+        sort_x(2, 1)
+        sort_g(1, 0, 1, v_copy)
+        sort_g(1, 1, 2, s_copy)
+        issue_loads()
+        for it in range(1, ROUNDS + 1):
+            if it - 1 in T_PAIRS:
                 quantise_g(it - 1)
-            if has_x(it - 1):
-                quantise_x(it - 1)
-            if has_x(it + 1):
-                sort_x(it + 1)
-            if has_g(it + 1) and it >= 0:
-                sort_g(it + 1)
-            if on_vector(it + 3):
-                sort_v(2 * (it + 3), nc.vector.tensor_copy)
-            if on_vector(it + 2):
-                turn_v(2 * (it + 2))
-            if on_vector(it + 1):
-                turn_v(2 * (it + 1) + 1)
+            if it < STAGES:
+                quantise_stage(it)
+            for r in turn_at.get(it - 2, []):
+                quantise_v(r)
+            if it + 2 < STAGES:
+                sort_x(it + 2, 1)
             issue_loads()
-            if has_x(it):
-                transpose_x(it)
-                if it < 1:
-                    keep_warm(4)
-            if has_g(it):
-                transpose_g(it)
-                if it < 1:
-                    keep_warm(4)
-            if it == ROUNDS:
+            if it + 1 < STAGES:
+                transpose_x(it + 1)
+            if it in T_PAIRS:
+                transpose_g(it, 0)
+                transpose_g(it, 1)
+            if it == 16:
                 last = [tp_pool.tile([P, 512], F32, name="xb%d" % h) for h in range(2)]
-                last_tap(0, 0, 8)
-            if exists_g(it - 1):
-                multiply(it - 1)
-            if on_vector(it):
-                merge_v(2 * it)
-            if has_x(it):
-                copy_x(it)
-            if on_vector(it):
-                merge_v(2 * it + 1)
-            if has_g(it):
-                copy_g(it)
-            if on_vector(it + 2):
-                sort_v(2 * (it + 2) + 1, nc.scalar.copy)
-
+            for h, r0, r1 in {16: [(0, 0, 8)]}.get(it, []):
+                last_tap(h, r0, r1)
+            if True:
+                for m in range(max(0, 4 * (it - 1) - 1), 4 * it - 1 if it < ROUNDS else 4 * it):
+                    multiply(m // 2, m % 2)
+            if it + 1 < STAGES:
+                copy_x(it + 1)
+                middle_tap(it + 1, both)
+            if it + 1 in T_PAIRS:
+                if it + 1 in sorted_by_scalar:
+                    sort_g(it + 1, 0, 1, v_copy)
+                else:
+                    sort_g(it + 1, 0, 2, v_copy)
+            for r in turn_at.get(it, []):
+                turn_v(r)
+            if it in T_PAIRS:
+                copy_g(it, 0, s_copy)
+                copy_g(it, 1, s_copy)
+            for r in turn_at.get(it - 1, []):
+                merge_v(r, s_copy)
+            if it >= 0 and it + 1 in T_PAIRS and it + 1 in sorted_by_scalar:
+                sort_g(it + 1, 1, 2, s_copy)
+            for r in turn_at.get(it + 1, []):
+                sort_v(r, s_copy)
         res = [keep.tile([P, GROUPS, CG, 9], F32, name="res%d" % h) for h in range(2)]
 
         def leave(h, dst, src):

@@ -26,7 +26,7 @@ GROUPS = 2
 CG = CI // GROUPS
 TAPW = 3 * CI
 X_SETS = [(u, min(u + 4, UNITS)) for u in range(0, UNITS, 4)]
-SETS = [(0, 4, "g"), (4, 8, "g"), (8, 12, "g"), (12, 14, "g"), (14, 16, "v"), (16, 18, "g"), (18, 20, "v"), (20, 22, "g"), (22, 24, "v"), (24, 26, "g"), (26, 28, "v"), (28, 30, "g"), (30, 32, "v")]
+SETS = [(0, 4, "g"), (4, 8, "g"), (8, 10, "g"), (10, 12, "v"), (12, 14, "g"), (14, 16, "v"), (16, 18, "g"), (18, 20, "v"), (20, 22, "g"), (22, 24, "v"), (24, 26, "g"), (26, 28, "v"), (28, 30, "g"), (30, 32, "v")]
 G_SETS = [s[:2] for s in SETS if s[2] == "g"]
 V_SETS = [s[:2] for s in SETS if s[2] == "v"]
 T_PAIRS = [r // 2 for lo, hi in G_SETS for r in range(lo, hi, 2)]
@@ -101,7 +101,7 @@ def tile_model_pa_kernel(tc, x, g, out):
             return vn
 
         load = {"x": load_x, "g": load_g, "v": load_v}
-        waiting = [("x", 0), ("g", 0), ("x", 1), ("g", 1), ("x", 2), ("g", 2), ("x", 3), ("v", 0), ("g", 3), ("x", 4), ("v", 1), ("g", 4), ("x", 5), ("v", 2), ("g", 5), ("x", 6), ("v", 3), ("g", 6), ("x", 7), ("v", 4), ("g", 7), ("x", 8)]
+        waiting = [("x", 0), ("g", 0), ("x", 1), ("g", 1), ("x", 2), ("v", 0), ("g", 2), ("x", 3), ("v", 1), ("g", 3), ("x", 4), ("v", 2), ("g", 4), ("x", 5), ("v", 3), ("g", 5), ("x", 6), ("v", 4), ("g", 6), ("x", 7), ("v", 5), ("g", 7), ("x", 8)]
 
         def issue_loads():
             while waiting:
@@ -119,7 +119,7 @@ def tile_model_pa_kernel(tc, x, g, out):
             xn, u0 = find("x", 2 * k)
             units = 2 * stages
             done["x"] = 2 * k + units
-            xr = rl_pool.tile([P, units, 3, P], F32, name="xr%d" % units)
+            xr = gr_pool.tile([P, units, 3, P], F32, name="xr%d" % units)
             for i in range(stages):
                 xs[k + i] = {"xr": xr, "lu": 2 * i}
             rows = xn[:].bitcast(F32)[:, :, :, u0 * XW : (u0 + units) * XW].rearrange(
@@ -140,7 +140,9 @@ def tile_model_pa_kernel(tc, x, g, out):
                 xb = tp_pool.tile([P, 512], F32, name=bank % lu)
                 xs[k]["xb"].append(xb)
                 for w in range(3):
-                    nc.tensor.transpose(xb[:, w * P : (w + 1) * P], xs[k]["xr"][:, xs[k]["lu"] + lu, w, :], ident[:])
+                    nc.tensor.transpose(
+                        xb[:, w * P : (w + 1) * P], xs[k]["xr"][:, xs[k]["lu"] + lu, w, :], ident[:]
+                    )
 
         def copy_x(k, unit=None, copy=nc.scalar.copy):
             if "xg" not in xs[k]:
@@ -191,7 +193,7 @@ def tile_model_pa_kernel(tc, x, g, out):
             done["g"] = 2 * q + li1
             if q not in gs:
                 gr = rl_pool.tile([P, 2, 2, 2, P], F32, name="gr")
-                gg = gr_pool.tile([P, 2, CO, 4], BF16, name="gg", align_bytes=64)
+                gg = gr_pool.tile([P, 2, 2, P, 4], BF16, name="gg", align_bytes=64)
                 gs[q] = {"gr": gr, "gg": gg}
             copy(
                 out=gs[q]["gr"][:, li0:li1, :, h0:h1].rearrange("p i w h (x b) -> p i w (h x) b", b=16),
@@ -200,18 +202,18 @@ def tile_model_pa_kernel(tc, x, g, out):
                 ),
             )
 
-        def transpose_g(q, li):
-            gb = tp_pool.tile([P, 512], F32, name="gb%d" % li)
-            gs[q]["gb", li] = gb
-            for w in range(2):
-                for h in range(2):
-                    k = 2 * w + h
+        def transpose_g(q, h, bank="gb%d"):
+            gb = tp_pool.tile([P, 512], F32, name=bank % h)
+            gs[q]["gb", h] = gb
+            for li in range(2):
+                for w in range(2):
+                    k = 2 * li + w
                     nc.tensor.transpose(gb[:, k * P : (k + 1) * P], gs[q]["gr"][:, li, w, h, :], ident[:])
 
-        def copy_g(q, li, copy):
+        def copy_g(q, h, copy):
             copy(
-                out=gs[q]["gg"][:].bitcast(F32)[:, li],
-                in_=gs[q]["gb", li][:].rearrange("p (w c) -> p c w", w=2),
+                out=gs[q]["gg"][:].bitcast(F32)[:, h],
+                in_=gs[q]["gb", h][:].rearrange("p (i w c) -> p i c w", i=2, w=2),
             )
 
         def quantise(gg, c0, width):
@@ -222,7 +224,14 @@ def tile_model_pa_kernel(tc, x, g, out):
             )
 
         def quantise_g(q):
-            quantise(gs[q]["gg"][:].rearrange("p i c t -> p (i c t)"), 2 * q * CO, 2 * CO)
+            quantise(gs[q]["gg"][:].rearrange("p h i c t -> p (h i c t)"), 2 * q * CO, 2 * CO)
+
+        def quantise_half(q, h):
+            quantise(gs[q]["gg"][:, h].rearrange("p i c t -> p (i c t)"), (2 * q + h) * CO, CO)
+
+        def g_column(r, h):
+            q, li = divmod(r, 2)
+            return q * 2 * CO + (h * CO + li * P if q in T_PAIRS else li * CO + h * P)
 
         def sort_v(r, copy):
             vn, l0 = find("v", r)
@@ -248,7 +257,7 @@ def tile_model_pa_kernel(tc, x, g, out):
             quantise(vs[r]["gv"][:].rearrange("p c t -> p (c t)"), r * CO, CO)
 
         def mx_pass(dst, r, h, col, width):
-            gc = r * CO + h * P
+            gc = g_column(r, h)
             xc = r * TAPW + col
             nc.tensor.matmul_mx(
                 out=dst,
@@ -277,8 +286,8 @@ def tile_model_pa_kernel(tc, x, g, out):
         v_copy = nc.vector.tensor_copy
         s_copy = nc.scalar.copy
         both = (0, 1)
-        turn_at = {5: [14], 6: [15], 7: [18], 8: [19], 9: [22], 10: [23], 11: [26], 12: [27], 13: [30], 14: [31]}
-        sorted_by_scalar = (3, 4, 5, 6, 8, 10, 12, 14,)
+        turn_at = {3: [10], 4: [11], 5: [14], 6: [15], 7: [18], 8: [19], 9: [22], 10: [23], 11: [26], 12: [27], 13: [30], 14: [31]}
+        sorted_by_scalar = (3, 4, 6, 8, 10, 12, 14,)
         sort_x(0, 1)
         sort_x(1, 1)
         issue_loads()
@@ -304,18 +313,24 @@ def tile_model_pa_kernel(tc, x, g, out):
         sort_g(1, 0, 1, v_copy)
         sort_g(1, 1, 2, s_copy)
         issue_loads()
+        x_at = {it: [it + 1] for it in range(1, STAGES - 1)}
+        for it in ():
+            x_at[it] = [it + 1, it + 2]
+            x_at[it + 1] = [it + 3]
+            x_at[it + 2] = []
         for it in range(1, ROUNDS + 1):
+            stages = x_at.get(it, [])
             if it - 1 in T_PAIRS:
                 quantise_g(it - 1)
-            if it < STAGES:
-                quantise_stage(it)
+            for k in x_at.get(it - 1, [1] if it == 1 else []):
+                quantise_stage(k)
             for r in turn_at.get(it - 2, []):
                 quantise_v(r)
-            if it + 2 < STAGES:
-                sort_x(it + 2, 1)
+            for k in x_at.get(it + 1, []):
+                sort_x(k, 1)
             issue_loads()
-            if it + 1 < STAGES:
-                transpose_x(it + 1)
+            for k in stages:
+                transpose_x(k, "xb%d" if k == stages[0] else "gb%d")
             if it in T_PAIRS:
                 transpose_g(it, 0)
                 transpose_g(it, 1)
@@ -326,9 +341,10 @@ def tile_model_pa_kernel(tc, x, g, out):
             if True:
                 for m in range(max(0, 4 * (it - 1) - 1), 4 * it - 1 if it < ROUNDS else 4 * it):
                     multiply(m // 2, m % 2)
-            if it + 1 < STAGES:
-                copy_x(it + 1)
-                middle_tap(it + 1, both)
+            for k in stages:
+                copy_x(k)
+            for k in stages:
+                middle_tap(k, both)
             if it + 1 in T_PAIRS:
                 if it + 1 in sorted_by_scalar:
                     sort_g(it + 1, 0, 1, v_copy)

@@ -303,7 +303,7 @@ def tile_model_pa_kernel(tc, x, g, out):
         keep_warm(2)
         transpose_g(0, 0)
         transpose_g(0, 1)
-        keep_warm(2)
+        keep_warm(4)
         quantise_stage(0)
         copy_x(1)
         copy_g(0, 0, s_copy)

from contextlib import ExitStack

import concourse.mybir as mybir
from concourse.masks import make_identity

F32 = mybir.dt.float32
BF16 = mybir.dt.bfloat16
U32 = mybir.dt.uint32
U8 = mybir.dt.uint8
FP8X4 = mybir.dt.float8_e4m3fn_x4

P = 128
N_IMG = 4
CI = 128
CO = 256
W_IN = 66
W_OUT = 64
HALF = 32
PASSES = 32
UNITS = 34
XW = W_IN // 2
GW = W_OUT // 2
ROUNDS = PASSES // 2
STAGES = UNITS // 2
GROUPS = 2
CG = CI // GROUPS
TAPW = 3 * CI
X_SETS = [(u, min(u + 4, UNITS)) for u in range(0, UNITS, 4)]
SETS = [(0, 4, "g"), (4, 8, "g"), (8, 10, "g"), (10, 12, "v"), (12, 14, "g"), (14, 16, "v"), (16, 18, "g"), (18, 20, "v"), (20, 22, "g"), (22, 24, "v"), (24, 26, "g"), (26, 28, "v"), (28, 30, "g"), (30, 32, "v")]
G_SETS = [s[:2] for s in SETS if s[2] == "g"]
V_SETS = [s[:2] for s in SETS if s[2] == "v"]
T_PAIRS = [r // 2 for lo, hi in G_SETS for r in range(lo, hi, 2)]
V_ROWS = [r for lo, hi in V_SETS for r in range(lo, hi)]
BUFS = {"x": 3, "g": 3, "v": 3}

FLOPS = 2 * CO * CI * 9 * N_IMG * W_OUT * W_OUT


def tile_model_pa_kernel(tc, x, g, out):
    nc = tc.nc
    with ExitStack() as ctx:
        keep = ctx.enter_context(tc.tile_pool(name="keep", bufs=1))
        xn_pool = ctx.enter_context(tc.tile_pool(name="xnp", bufs=BUFS["x"]))
        gn_pool = ctx.enter_context(tc.tile_pool(name="gnp", bufs=BUFS["g"]))
        vn_pool = ctx.enter_context(tc.tile_pool(name="vnp", bufs=BUFS["v"]))
        v_pool = ctx.enter_context(tc.tile_pool(name="vp", bufs=2))
        rl_pool = ctx.enter_context(tc.tile_pool(name="rl", bufs=2))
        gr_pool = ctx.enter_context(tc.tile_pool(name="grp", bufs=3))
        acc_pool = ctx.enter_context(tc.psum_pool(name="acc", bufs=1))
        tp_pool = ctx.enter_context(tc.psum_pool(name="tp", bufs=1))
        ctx.enter_context(tc.manual_schedule())

        blank = keep.tile([P, 512], BF16, name="blank")
        nc.vector.memset(blank[:], 0.0)
        ident = keep.tile([P, P], F32, name="ident")
        make_identity(nc, ident[:])

        g_codes = keep.tile([P, PASSES * CO], U32, name="g_codes", align_bytes=64)
        g_scales = keep.tile([P, PASSES * CO], U8, name="g_scales", align_bytes=64)
        x_codes = keep.tile([P, UNITS * TAPW], U32, name="x_codes", align_bytes=64)
        x_scales = keep.tile([P, UNITS * TAPW], U8, name="x_scales", align_bytes=64)
        acc = [[acc_pool.tile([P, 512], F32, name="acc%d%d" % (h, s)) for s in range(2)] for h in range(2)]

        sets = {"x": X_SETS, "g": G_SETS, "v": V_SETS}
        tiles = {}
        done = {"x": 0, "g": 0, "v": 0}
        xs = {}
        gs = {}
        vs = {}

        def load_x(u0, u1):
            run = (u1 - u0) * W_IN
            xn = xn_pool.tile([P, N_IMG, 2, (run + 15) // 16 * 16], BF16, name="xn")
            for a in range(2):
                nc.sync.dma_start(
                    out=xn[:, :, a, 0:run],
                    in_=x[:, :, HALF * a + u0 : HALF * a + u1, :].rearrange("n c h w -> c n (h w)"),
                )
            return xn

        def load_g(r0, r1):
            gn = gn_pool.tile([P, 2, N_IMG, 2, (r1 - r0) * W_OUT], BF16, name="gn")
            for h in range(2):
                for a in range(2):
                    nc.sync.dma_start(
                        out=gn[:, h, :, a, :],
                        in_=g[:, P * h : P * (h + 1), HALF * a + r0 : HALF * a + r1, :].rearrange(
                            "n c h w -> c n (h w)"
                        ),
                    )
            return gn

        def load_v(r0, r1):
            vn = vn_pool.tile([P, CO // 32, 2, (r1 - r0) * W_OUT], BF16, name="vn")
            for n in (0, 2, 1, 3):
                for a in range(2):
                    nc.sync.dma_start(
                        out=vn[32 * n : 32 * n + 32, :, a, :],
                        in_=g[n, :, HALF * a + r0 : HALF * a + r1, :].rearrange("(k c) h w -> c k (h w)", c=32),
                    )
            return vn

        load = {"x": load_x, "g": load_g, "v": load_v}
        waiting = [("x", 0), ("g", 0), ("x", 1), ("g", 1), ("x", 2), ("v", 0), ("g", 2), ("x", 3), ("v", 1), ("g", 3), ("x", 4), ("v", 2), ("g", 4), ("x", 5), ("v", 3), ("g", 5), ("x", 6), ("v", 4), ("g", 6), ("x", 7), ("v", 5), ("g", 7), ("x", 8)]

        def issue_loads():
            while waiting:
                kind, i = waiting[0]
                if i >= BUFS[kind] and done[kind] < sets[kind][i - BUFS[kind]][1]:
                    return
                waiting.remove(waiting[0])
                tiles[kind, i] = load[kind](*sets[kind][i])

        def find(kind, first):
            i = max(i for i, (lo, hi) in enumerate(sets[kind]) if lo <= first)
            return tiles[kind, i], first - sets[kind][i][0]

        def sort_x(k, stages):
            xn, u0 = find("x", 2 * k)
            units = 2 * stages
            done["x"] = 2 * k + units
            xr = gr_pool.tile([P, units, 3, P], F32, name="xr%d" % units)
            for i in range(stages):
                xs[k + i] = {"xr": xr, "lu": 2 * i}
            rows = xn[:].bitcast(F32)[:, :, :, u0 * XW : (u0 + units) * XW].rearrange(
                "p n a (u k) -> p u (n a) k", u=units, k=XW
            )
            nc.vector.tensor_copy(
                out=xr[:, :, 0:2, :].rearrange("p u w (x b) -> p u w x b", b=16),
                in_=rows[:, :, :, 0:32].rearrange("p u x (b w) -> p u w x b", w=2),
            )
            (nc.scalar.copy if k in range(5, 17, 2) else nc.vector.tensor_copy)(
                out=xr[:, :, 2, :].rearrange("p u (x b) -> p u x b", b=16),
                in_=rows[:, :, :, 2:33:2],
            )

        def transpose_x(k, bank="xb%d"):
            xs[k]["xb"] = []
            for lu in range(2):
                xb = tp_pool.tile([P, 512], F32, name=bank % lu)
                xs[k]["xb"].append(xb)
                for w in range(3):
                    nc.tensor.transpose(
                        xb[:, w * P : (w + 1) * P], xs[k]["xr"][:, xs[k]["lu"] + lu, w, :], ident[:]
                    )

        def copy_x(k, unit=None, copy=nc.scalar.copy):
            if "xg" not in xs[k]:
                xg = gr_pool.tile([P, 2, GROUPS, 3, CG, 4], BF16, name="xg", align_bytes=64)
                xs[k]["xg"] = xg
            xg_w = xs[k]["xg"][:].bitcast(F32)
            for lu in range(2) if unit is None else (unit,):
                for j in range(2):
                    copy(
                        out=xg_w[:, lu, :, 2 * j],
                        in_=xs[k]["xb"][lu][:, j * P : (j + 2) * P].rearrange("p (w g c) -> p g c w", w=2, g=GROUPS),
                    )

        def middle_tap(k, units, on_scalar=False):
            flat = xs[k]["xg"][:].rearrange("p u g k c t -> p (u g) k c t")
            blocks = range(GROUPS * units[0], GROUPS * (units[-1] + 1))
            if on_scalar:
                for v in blocks:
                    nc.scalar.copy(
                        out=flat[:, v, 1].rearrange("p c (k e) -> p c k e", k=2),
                        in_=flat[:, v, 0:3:2, :, 1:3].rearrange("p k c e -> p c k e"),
                    )
            else:
                bs = slice(blocks[0], blocks[-1] + 1)
                nc.vector.tensor_copy(
                    out=flat[:, bs, 1].rearrange("p v c (k e) -> p v c k e", k=2),
                    in_=flat[:, bs, 0:3:2, :, 1:3].rearrange("p v k c e -> p v c k e"),
                )

        def quantise_x(k, lo, hi):
            c0 = 2 * k * TAPW
            nc.vector.quantize_mx(
                out=x_codes[:, c0 + lo : c0 + hi].bitcast(FP8X4),
                scales=x_scales[:, c0 + lo : c0 + hi],
                in_=xs[k]["xg"][:].rearrange("p u g k c t -> p (u g k c t)")[:, 4 * lo : 4 * hi],
            )

        def quantise_stage(k):
            quantise_x(k, 0, 512)
            quantise_x(k, 512, 768)

        def quantise_unit(k, u):
            quantise_x(k, 384 * u, 384 * u + 256)
            quantise_x(k, 384 * u + 256, 384 * u + 384)

        def sort_g(q, li0, li1, copy, h0=0, h1=2):
            gn, l0 = find("g", 2 * q)
            done["g"] = 2 * q + li1
            if q not in gs:
                gr = rl_pool.tile([P, 2, 2, 2, P], F32, name="gr")
                gg = gr_pool.tile([P, 2, 2, P, 4], BF16, name="gg", align_bytes=64)
                gs[q] = {"gr": gr, "gg": gg}
            copy(
                out=gs[q]["gr"][:, li0:li1, :, h0:h1].rearrange("p i w h (x b) -> p i w (h x) b", b=16),
                in_=gn[:].bitcast(F32)[:, h0:h1, :, :, (l0 + li0) * GW : (l0 + li1) * GW].rearrange(
                    "p h n a (i b w) -> p i w (h n a) b", i=li1 - li0, b=16, w=2
                ),
            )

        def transpose_g(q, h, bank="gb%d"):
            gb = tp_pool.tile([P, 512], F32, name=bank % h)
            gs[q]["gb", h] = gb
            for li in range(2):
                for w in range(2):
                    k = 2 * li + w
                    nc.tensor.transpose(gb[:, k * P : (k + 1) * P], gs[q]["gr"][:, li, w, h, :], ident[:])

        def copy_g(q, h, copy):
            copy(
                out=gs[q]["gg"][:].bitcast(F32)[:, h],
                in_=gs[q]["gb", h][:].rearrange("p (i w c) -> p i c w", i=2, w=2),
            )

        def quantise(gg, c0, width):
            nc.vector.quantize_mx(
                out=g_codes[:, c0 : c0 + width].bitcast(FP8X4),
                scales=g_scales[:, c0 : c0 + width],
                in_=gg,
            )

        def quantise_g(q):
            quantise(gs[q]["gg"][:].rearrange("p h i c t -> p (h i c t)"), 2 * q * CO, 2 * CO)

        def quantise_half(q, h):
            quantise(gs[q]["gg"][:, h].rearrange("p i c t -> p (i c t)"), (2 * q + h) * CO, CO)

        def g_column(r, h):
            q, li = divmod(r, 2)
            return q * 2 * CO + (h * CO + li * P if q in T_PAIRS else li * CO + h * P)

        def sort_v(r, copy):
            vn, l0 = find("v", r)
            done["v"] = r + 1
            ds = v_pool.tile([P, 2, CO // 16, 16], F32, name="ds", align_bytes=64)
            vs[r] = {"ds": ds}
            copy(
                out=ds[:],
                in_=vn[:].bitcast(F32)[:, :, :, l0 * GW : (l0 + 1) * GW].rearrange("p k a (b w) -> p w (k a) b", w=2),
            )

        def turn_v(r):
            dt = v_pool.tile([P, 2 * CO], F32, name="dt", align_bytes=64)
            vs[r]["dt"] = dt
            nc.vector.transpose(out=dt[:], in_=vs[r]["ds"][:].rearrange("p w x b -> p (w x b)"))

        def merge_v(r, copy):
            gv = gr_pool.tile([P, CO, 4], BF16, name="gv", align_bytes=64)
            vs[r]["gv"] = gv
            copy(out=gv[:].bitcast(F32), in_=vs[r]["dt"][:].rearrange("p (w c) -> p c w", w=2))

        def quantise_v(r):
            quantise(vs[r]["gv"][:].rearrange("p c t -> p (c t)"), r * CO, CO)

        def mx_pass(dst, r, h, col, width):
            gc = g_column(r, h)
            xc = r * TAPW + col
            nc.tensor.matmul_mx(
                out=dst,
                lhsT=g_codes[:, gc : gc + P].bitcast(FP8X4),
                lhsT_scale=g_scales[:, gc : gc + P],
                rhs=x_codes[:, xc : xc + width].bitcast(FP8X4),
                rhs_scale=x_scales[:, xc : xc + width],
                start=(r == 0),
                stop=(r == PASSES - 1),
            )

        def multiply(r, s, halves=(0, 1)):
            for h in halves:
                mx_pass(acc[h][s][:], r, h, 512 * s, 512)

        def last_tap(h, r0, r1):
            for r in range(r0, r1):
                mx_pass(last[h][:, 0:P], r, h, 1024, P)

        def keep_warm(passes):
            for i in range(passes):
                nc.tensor.matmul(acc[0][0][:], lhsT=blank[:, 0:P], rhs=blank[:], start=True, stop=True)

        issue_loads()
        keep_warm(8)
        v_copy = nc.vector.tensor_copy
        s_copy = nc.scalar.copy
        both = (0, 1)
        turn_at = {3: [10], 4: [11], 5: [14], 6: [15], 7: [18], 8: [19], 9: [22], 10: [23], 11: [26], 12: [27], 13: [30], 14: [31]}
        sorted_by_scalar = (3, 4, 6, 8, 10, 12, 14,)
        sort_x(0, 1)
        sort_x(1, 1)
        issue_loads()
        transpose_x(0)
        keep_warm(3)
        copy_x(0)
        sort_g(0, 0, 2, v_copy, 0, 1)
        middle_tap(0, (0,), True)
        middle_tap(0, (1,))
        sort_g(0, 0, 2, v_copy, 1, 2)
        issue_loads()
        transpose_x(1)
        keep_warm(2)
        transpose_g(0, 0)
        transpose_g(0, 1)
        keep_warm(4)
        quantise_stage(0)
        copy_x(1)
        copy_g(0, 0, s_copy)
        copy_g(0, 1, s_copy)
        middle_tap(1, both)
        sort_x(2, 1)
        sort_g(1, 0, 1, v_copy)
        sort_g(1, 1, 2, s_copy)
        issue_loads()
        x_at = {it: [it + 1] for it in range(1, STAGES - 1)}
        for it in ():
            x_at[it] = [it + 1, it + 2]
            x_at[it + 1] = [it + 3]
            x_at[it + 2] = []
        for it in range(1, ROUNDS + 1):
            stages = x_at.get(it, [])
            if it - 1 in T_PAIRS:
                quantise_g(it - 1)
            for k in x_at.get(it - 1, [1] if it == 1 else []):
                quantise_stage(k)
            for r in turn_at.get(it - 2, []):
                quantise_v(r)
            for k in x_at.get(it + 1, []):
                sort_x(k, 1)
            issue_loads()
            for k in stages:
                transpose_x(k, "xb%d" if k == stages[0] else "gb%d")
            if it in T_PAIRS:
                transpose_g(it, 0)
                transpose_g(it, 1)
            if it == 16:
                last = [tp_pool.tile([P, 512], F32, name="xb%d" % h) for h in range(2)]
            for h, r0, r1 in {16: [(0, 0, 8)]}.get(it, []):
                last_tap(h, r0, r1)
            if True:
                for m in range(max(0, 4 * (it - 1) - 1), 4 * it - 1 if it < ROUNDS else 4 * it):
                    multiply(m // 2, m % 2)
            for k in stages:
                copy_x(k)
            for k in stages:
                middle_tap(k, both)
            if it + 1 in T_PAIRS:
                if it + 1 in sorted_by_scalar:
                    sort_g(it + 1, 0, 1, v_copy)
                else:
                    sort_g(it + 1, 0, 2, v_copy)
            for r in turn_at.get(it, []):
                turn_v(r)
            if it in T_PAIRS:
                copy_g(it, 0, s_copy)
                copy_g(it, 1, s_copy)
            for r in turn_at.get(it - 1, []):
                merge_v(r, s_copy)
            if it >= 0 and it + 1 in T_PAIRS and it + 1 in sorted_by_scalar:
                sort_g(it + 1, 1, 2, s_copy)
            for r in turn_at.get(it + 1, []):
                sort_v(r, s_copy)
        res = [keep.tile([P, GROUPS, CG, 9], F32, name="res%d" % h) for h in range(2)]

        def leave(h, dst, src):
            copy = nc.vector.tensor_copy if h == 0 else nc.scalar.copy
            copy(out=dst, in_=src)

        def store(h, g, c0, c1):
            nc.sync.dma_start(
                out=out[h * P : (h + 1) * P, CG * g + c0 : CG * g + c1].rearrange("o c kh kw -> o (c kh kw)"),
                in_=res[h][:, g, c0:c1].rearrange("p c t -> p (c t)"),
            )

        for h in range(2):
            leave(h, res[h][:, 0, :, 0:3], acc[h][0][:, 0 : 3 * CG].rearrange("p (t c) -> p c t", t=3))
            leave(h, res[h][:, 0, :, 3:5], acc[h][0][:, 6 * CG : 8 * CG].rearrange("p (t c) -> p c t", t=2))
            leave(h, res[h][:, 0, :, 5:6], acc[h][1][:, 0:CG].rearrange("p (t c) -> p c t", t=1))
            leave(h, res[h][:, 0, :, 6:9], acc[h][1][:, 4 * CG : 7 * CG].rearrange("p (t c) -> p c t", t=3))
            store(h, 0, 0, CG)
        for h in range(2):
            leave(h, res[h][:, 1, :, 0:3], acc[h][0][:, 3 * CG : 6 * CG].rearrange("p (t c) -> p c t", t=3))
            leave(h, res[h][:, 1, :, 3:6], acc[h][1][:, CG : 4 * CG].rearrange("p (t c) -> p c t", t=3))
            leave(h, res[h][:, 1, :, 6:7], acc[h][1][:, 7 * CG : 8 * CG].rearrange("p (t c) -> p c t", t=1))
        last_tap(0, 8, PASSES)
        last_tap(1, 0, PASSES)
        for h in range(2):
            left = last[h][:, 0:P].rearrange("p (t c) -> p t c", t=2)
            for c0 in range(0, CG, CG // 2):
                c1 = c0 + CG // 2
                leave(h, res[h][:, 1, c0:c1, 7:9], left[:, :, c0:c1].rearrange("p t c -> p c t"))
                store(h, 1, c0, c1)
